import numpy as np
import ml_dtypes


def mxq(x, axis, fmt="e4m3"):
    dtype, down = {"e4m3": (ml_dtypes.float8_e4m3fn, 7), "e5m2": (ml_dtypes.float8_e5m2, 14)}[fmt]
    v = np.moveaxis(np.asarray(x, np.float32).astype(ml_dtypes.bfloat16).astype(np.float64), axis, -1)
    blocks = v.reshape(v.shape[:-1] + (-1, 32))
    amax = np.abs(blocks).max(-1, keepdims=True)
    byte = np.maximum(np.where(amax > 0, np.frexp(amax)[1] - 1 + 127, 0) - down, 1)
    scale = np.exp2(byte - 127.0)
    codes = (blocks / scale).astype(np.float32).astype(dtype).astype(np.float64)
    return np.moveaxis((codes * scale).reshape(v.shape), -1, axis)


WIDE = False


def mx_kscale(k):
    if not WIDE:
        return np.ones(k)
    levels = np.array([10, -10, 5, -5, 0])
    a = np.random.permutation(np.resize(levels, k // 512 * 4)).reshape(k // 512, 4)
    idx = np.arange(k)
    return np.exp2(a[idx // 512, idx % 128 // 32])


BF16 = ml_dtypes.bfloat16


def bf(x):
    return np.asarray(x, np.float32).astype(BF16)


def f64(x):
    return np.asarray(x).astype(np.float64)


B, S, E, H, KD, HD, C = 1, 1024, 1024, 8, 128, 256, 512
V = H * HD
EPS = 1e-5


def silu(v):
    return v / (1.0 + np.exp(-v))


def setup_inputs():
    s = mx_kscale(E)
    lvl = np.exp2(np.random.uniform(-9.0, 2.0, (B, S, H, 1)))
    return {"x": bf(np.random.standard_normal((B, S, E)) * s),
            "wg": bf(np.random.standard_normal((E, V)) / np.sqrt(E) / s[:, None]),
            "ret": bf(np.random.standard_normal((B, S, H, HD)) * lvl),
            "wo": bf(np.random.standard_normal((V, E)) * 1.5 / np.sqrt(V))}


def reference(x, wg, ret, wo):
    g = mxq(f64(x), 2, "e4m3") @ mxq(f64(wg), 0, "e4m3")
    r = f64(ret)
    n = r * (1.0 / np.sqrt(np.mean(r * r, axis=-1, keepdims=True) + EPS))
    h = silu(g) * n.reshape(B, S, V)
    return mxq(h, 2, "e4m3") @ mxq(f64(wo), 0, "e4m3")

@@ -1,0 +1,264 @@
+import concourse.mybir as mybir
+from concourse.masks import make_identity
+
+F32 = mybir.dt.float32
+BF16 = mybir.dt.bfloat16
+U32 = mybir.dt.uint32
+U8 = mybir.dt.uint8
+FP8X4 = mybir.dt.float8_e4m3fn_x4
+ACT = mybir.ActivationFunctionType
+ALU = mybir.AluOpType
+
+P = 128
+S, E, V = 1024, 1024, 2048
+HEADS, HEAD_DIM = 8, 256
+EPS = 1e-5
+PACK = 4
+K_PASS = P * PACK
+N_TILE = 512
+S_TILES = S // P
+E_PASSES = E // K_PASS
+V_PASSES = V // K_PASS
+V_CHUNKS = V // N_TILE
+E_CHUNKS = E // N_TILE
+HEADS_PER_CHUNK = N_TILE // HEAD_DIM
+FIRST_GROUP = 4
+FLOPS = 2 * S * E * V + 2 * S * V * E
+
+
+def regroup(copy, grouped, planes):
+    copy(
+        out=grouped.rearrange("p (c i t) -> p c t i", i=4, t=PACK),
+        in_=planes.rearrange("p t (c i) -> p c t i", i=4),
+    )
+
+
+def tile_retnet_pc_kernel(tc, x, wg, ret, wo, out):
+    nc = tc.nc
+    x_rows = x.flatten_outer_dims()
+    ret_rows = ret.rearrange("b s h d -> (b s) (h d)")
+    out_rows = out.flatten_outer_dims()
+    wg_by_parity = wg.rearrange("(a q e) v -> e q a v", a=2 * E_PASSES, q=P, e=2)
+
+    with (
+        tc.tile_pool(name="const", bufs=1) as const,
+        tc.tile_pool(name="x_in", bufs=S_TILES) as x_in,
+        tc.tile_pool(name="ret_in", bufs=S_TILES) as ret_in,
+        tc.tile_pool(name="w_in", bufs=4) as w_in,
+        tc.tile_pool(name="keep", bufs=1) as keep,
+        tc.tile_pool(name="group", bufs=3) as group,
+        tc.tile_pool(name="gate", bufs=18) as gate,
+        tc.tile_pool(name="stats", bufs=S_TILES) as stats,
+        tc.tile_pool(name="pairs", bufs=2) as pairs,
+        tc.tile_pool(name="work", bufs=2) as work,
+        tc.tile_pool(name="store", bufs=4) as store,
+        tc.psum_pool(name="g_banks", bufs=4) as g_banks,
+        tc.psum_pool(name="t_banks", bufs=2) as t_banks,
+        tc.psum_pool(name="o_banks", bufs=2) as o_banks,
+    ):
+        ident = const.tile([P, P], F32)
+        make_identity(nc, ident[:])
+        minus_half = const.tile([P, HEADS], F32)
+        nc.vector.memset(minus_half[:], -0.5)
+        squares = const.tile([P, V], BF16)
+
+        x_codes = keep.tile([P, S_TILES, E_PASSES * P], U32, align_bytes=64)
+        x_scales = keep.tile([P, S_TILES, E_PASSES * P], U8, align_bytes=64)
+        wg_codes = keep.tile([P, E_PASSES, V], U32, align_bytes=64)
+        wg_scales = keep.tile([P, E_PASSES, V], U8, align_bytes=64)
+        wo_codes = keep.tile([P, V_PASSES, E], U32, align_bytes=64)
+        wo_scales = keep.tile([P, V_PASSES, E], U8, align_bytes=64)
+
+        x_tiles, ret_tiles, wg_raws, wo_raws = {}, {}, {}, {}
+
+        def load_x(j):
+            x_sb = x_in.tile([P, E], BF16)
+            nc.sync.dma_start(out=x_sb[:], in_=x_rows[j * P : (j + 1) * P, :])
+            x_tiles[j] = x_sb
+
+        def load_ret(j):
+            ret_sb = ret_in.tile([P, V], BF16)
+            nc.sync.dma_start(out=ret_sb[:], in_=ret_rows[j * P : (j + 1) * P, :])
+            ret_tiles[j] = ret_sb
+
+        def load_wg(c):
+            w_raw = w_in.tile([P, E_PASSES * PACK * N_TILE], BF16)
+            planes = w_raw[:].rearrange("p (a e v) -> p a e v", a=2 * E_PASSES, e=2)
+            for e in range(2):
+                nc.sync.dma_start(
+                    out=planes[:, :, e, :],
+                    in_=wg_by_parity[e, :, :, c * N_TILE : (c + 1) * N_TILE],
+                )
+            wg_raws[c] = w_raw
+
+        def load_wo(c):
+            w_raw = w_in.tile([P, PACK * E], BF16)
+            nc.sync.dma_start(
+                out=w_raw[:].rearrange("p (u r) -> p u r", u=2),
+                in_=wo[c * K_PASS : (c + 1) * K_PASS, :].rearrange(
+                    "(u q e) n -> q u (e n)", u=2, q=P, e=2
+                ),
+            )
+            wo_raws[c] = w_raw
+
+        def quantise_x(j):
+            x_words = x_tiles[j][:].bitcast(F32)
+            x_t = t_banks.tile([P, N_TILE], F32, tag="t_bank")
+            for a in range(2 * E_PASSES):
+                nc.tensor.transpose(
+                    x_t[:, a * P : (a + 1) * P], x_words[:, a * P : (a + 1) * P], ident[:]
+                )
+            x_grouped = pairs.tile([P, E], BF16, align_bytes=64)
+            nc.scalar.copy(
+                out=x_grouped[:].bitcast(F32).rearrange("p (g s u) -> p g s u", g=E_PASSES, u=2),
+                in_=x_t[:].rearrange("p (g u s) -> p g s u", g=E_PASSES, u=2),
+            )
+            nc.vector.quantize_mx(
+                out=x_codes[:, j, :].bitcast(FP8X4), scales=x_scales[:, j, :], in_=x_grouped[:]
+            )
+
+        def quantise_wg(c):
+            planes = wg_raws[c][:].rearrange("p (g t v) -> p g t v", g=E_PASSES, t=PACK)
+            cols = slice(c * N_TILE, (c + 1) * N_TILE)
+            for g in range(E_PASSES):
+                grouped = group.tile([P, PACK * N_TILE], BF16, align_bytes=64)
+                regroup(nc.vector.tensor_copy, grouped[:], planes[:, g])
+                nc.vector.quantize_mx(
+                    out=wg_codes[:, g, cols].bitcast(FP8X4),
+                    scales=wg_scales[:, g, cols],
+                    in_=grouped[:],
+                )
+
+        def quantise_wo(c):
+            planes = wo_raws[c][:].rearrange("p (t n) -> p t n", t=PACK)
+            for n in range(E_CHUNKS):
+                cols = slice(n * N_TILE, (n + 1) * N_TILE)
+                grouped = group.tile([P, PACK * N_TILE], BF16, align_bytes=64)
+                regroup(nc.vector.tensor_copy, grouped[:], planes[:, :, cols])
+                nc.vector.quantize_mx(
+                    out=wo_codes[:, c, cols].bitcast(FP8X4),
+                    scales=wo_scales[:, c, cols],
+                    in_=grouped[:],
+                )
+
+        rstds, silus = {}, {}
+
+        def head_norms(j):
+            sumsq = stats.tile([P, HEADS], F32)
+            for h in range(HEADS):
+                cols = slice(h * HEAD_DIM, (h + 1) * HEAD_DIM)
+                nc.scalar.activation(
+                    out=squares[:, cols],
+                    in_=ret_tiles[j][:, cols],
+                    func=ACT.Square,
+                    accum_out=sumsq[:, h : h + 1],
+                )
+            meansq = stats.tile([P, HEADS], F32)
+            nc.gpsimd.tensor_scalar(
+                out=meansq[:], in0=sumsq[:], scalar1=1.0 / HEAD_DIM, scalar2=EPS,
+                op0=ALU.mult, op1=ALU.add,
+            )
+            rstd = stats.tile([P, HEADS], F32)
+            nc.gpsimd.tensor_tensor(out=rstd[:], in0=meansq[:], in1=minus_half[:], op=ALU.pow)
+            rstds[j] = rstd
+
+        def gate_chunk(j, c):
+            g_bank = g_banks.tile([P, N_TILE], F32)
+            for g in range(E_PASSES):
+                nc.tensor.matmul_mx(
+                    out=g_bank[:],
+                    lhsT=x_codes[:, j, g * P : (g + 1) * P].bitcast(FP8X4),
+                    lhsT_scale=x_scales[:, j, g * P : (g + 1) * P],
+                    rhs=wg_codes[:, g, c * N_TILE : (c + 1) * N_TILE].bitcast(FP8X4),
+                    rhs_scale=wg_scales[:, g, c * N_TILE : (c + 1) * N_TILE],
+                    start=(g == 0),
+                    stop=(g == E_PASSES - 1),
+                )
+            silu = gate.tile([P, N_TILE], F32)
+            nc.scalar.activation(out=silu[:], in_=g_bank[:], func=ACT.Silu)
+            silus[j, c] = silu
+
+        h_operands = {}
+
+        def quantise_h(j):
+            h_sb = work.tile([P, V], BF16)
+            for h in range(HEADS):
+                cols = slice(h * HEAD_DIM, (h + 1) * HEAD_DIM)
+                part = slice((h % HEADS_PER_CHUNK) * HEAD_DIM, (h % HEADS_PER_CHUNK + 1) * HEAD_DIM)
+                nc.vector.scalar_tensor_tensor(
+                    out=h_sb[:, cols],
+                    in0=silus[j, h // HEADS_PER_CHUNK][:, part],
+                    scalar=rstds[j][:, h : h + 1],
+                    in1=ret_tiles[j][:, cols],
+                    op0=ALU.mult,
+                    op1=ALU.mult,
+                )
+            h_words = h_sb[:].bitcast(F32)
+            h_grouped = pairs.tile([P, V], BF16, align_bytes=64)
+            h_grouped_words = h_grouped[:].bitcast(F32)
+            for b in range(2):
+                h_t = t_banks.tile([P, N_TILE], F32, tag="t_bank")
+                for a in range(4):
+                    w0 = (4 * b + a) * P
+                    nc.tensor.transpose(h_t[:, a * P : (a + 1) * P], h_words[:, w0 : w0 + P], ident[:])
+                nc.scalar.copy(
+                    out=h_grouped_words[:, b * N_TILE : (b + 1) * N_TILE].rearrange(
+                        "p (c s u) -> p c s u", c=2, u=2
+                    ),
+                    in_=h_t[:].rearrange("p (c u s) -> p c s u", c=2, u=2),
+                )
+            h_codes = work.tile([P, V_PASSES * P], U32, align_bytes=64)
+            h_scales = work.tile([P, V_PASSES * P], U8, align_bytes=64)
+            nc.vector.quantize_mx(out=h_codes[:].bitcast(FP8X4), scales=h_scales[:], in_=h_grouped[:])
+            h_operands[j] = (h_codes, h_scales)
+
+        def project(j):
+            h_codes, h_scales = h_operands[j]
+            for n in range(E_CHUNKS):
+                o_bank = o_banks.tile([P, N_TILE], F32)
+                for c in range(V_PASSES):
+                    nc.tensor.matmul_mx(
+                        out=o_bank[:],
+                        lhsT=h_codes[:, c * P : (c + 1) * P].bitcast(FP8X4),
+                        lhsT_scale=h_scales[:, c * P : (c + 1) * P],
+                        rhs=wo_codes[:, c, n * N_TILE : (n + 1) * N_TILE].bitcast(FP8X4),
+                        rhs_scale=wo_scales[:, c, n * N_TILE : (n + 1) * N_TILE],
+                        start=(c == 0),
+                        stop=(c == V_PASSES - 1),
+                    )
+                out_sb = store.tile([P, N_TILE], F32)
+                if n % 2 == 0:
+                    nc.vector.tensor_copy(out=out_sb[:], in_=o_bank[:])
+                else:
+                    nc.scalar.copy(out=out_sb[:], in_=o_bank[:])
+                nc.sync.dma_start(
+                    out=out_rows[j * P : (j + 1) * P, n * N_TILE : (n + 1) * N_TILE], in_=out_sb[:]
+                )
+
+        for j in range(FIRST_GROUP):
+            load_x(j)
+        for c in range(V_CHUNKS):
+            load_wg(c)
+            load_ret(c)
+
+        for j in range(FIRST_GROUP):
+            quantise_x(j)
+        for c in range(V_CHUNKS):
+            quantise_wg(c)
+            load_wo(c)
+            load_x(FIRST_GROUP + c)
+            load_ret(FIRST_GROUP + c)
+            for j in range(FIRST_GROUP):
+                gate_chunk(j, c)
+            head_norms(c)
+        for c in range(V_PASSES):
+            quantise_wo(c)
+        for j in range(S_TILES):
+            quantise_h(j)
+            later = j + FIRST_GROUP
+            if later < S_TILES:
+                quantise_x(later)
+                head_norms(later)
+                for c in range(V_CHUNKS):
+                    gate_chunk(later, c)
+            project(j)

@@ -23,6 +23,10 @@ V_CHUNKS = V // N_TILE
 E_CHUNKS = E // N_TILE
 HEADS_PER_CHUNK = N_TILE // HEAD_DIM
 FIRST_GROUP = 4
+WO_STEPS = 4
+NORMS_AHEAD = 2
+PROJECT_LAG = 3
+assert PROJECT_LAG >= WO_STEPS - 1
 FLOPS = 2 * S * E * V + 2 * S * V * E
 
 
@@ -49,8 +53,9 @@ def tile_retnet_pc_kernel(tc, x, wg, ret, wo, out):
         tc.tile_pool(name="group", bufs=3) as group,
         tc.tile_pool(name="gate", bufs=18) as gate,
         tc.tile_pool(name="stats", bufs=S_TILES) as stats,
-        tc.tile_pool(name="pairs", bufs=2) as pairs,
+        tc.tile_pool(name="pairs", bufs=3) as pairs,
         tc.tile_pool(name="work", bufs=2) as work,
+        tc.tile_pool(name="h_ops", bufs=5) as h_ops,
         tc.tile_pool(name="store", bufs=4) as store,
         tc.psum_pool(name="g_banks", bufs=4) as g_banks,
         tc.psum_pool(name="t_banks", bufs=2) as t_banks,
@@ -120,25 +125,31 @@ def tile_retnet_pc_kernel(tc, x, wg, ret, wo, out):
         def quantise_wg(c):
             planes = wg_raws[c][:].rearrange("p (g t v) -> p g t v", g=E_PASSES, t=PACK)
             cols = slice(c * N_TILE, (c + 1) * N_TILE)
+            groupeds = []
             for g in range(E_PASSES):
                 grouped = group.tile([P, PACK * N_TILE], BF16, align_bytes=64)
                 regroup(nc.vector.tensor_copy, grouped[:], planes[:, g])
+                groupeds.append(grouped)
+            for g in range(E_PASSES):
                 nc.vector.quantize_mx(
                     out=wg_codes[:, g, cols].bitcast(FP8X4),
                     scales=wg_scales[:, g, cols],
-                    in_=grouped[:],
+                    in_=groupeds[g][:],
                 )
 
-        def quantise_wo(c):
-            planes = wo_raws[c][:].rearrange("p (t n) -> p t n", t=PACK)
-            for n in range(E_CHUNKS):
-                cols = slice(n * N_TILE, (n + 1) * N_TILE)
+        def quantise_wo(n, passes):
+            cols = slice(n * N_TILE, (n + 1) * N_TILE)
+            groupeds = {}
+            for c in passes:
+                planes = wo_raws[c][:].rearrange("p (t n) -> p t n", t=PACK)
                 grouped = group.tile([P, PACK * N_TILE], BF16, align_bytes=64)
                 regroup(nc.vector.tensor_copy, grouped[:], planes[:, :, cols])
+                groupeds[c] = grouped
+            for c in passes:
                 nc.vector.quantize_mx(
                     out=wo_codes[:, c, cols].bitcast(FP8X4),
                     scales=wo_scales[:, c, cols],
-                    in_=grouped[:],
+                    in_=groupeds[c][:],
                 )
 
         rstds, silus = {}, {}
@@ -178,9 +189,9 @@ def tile_retnet_pc_kernel(tc, x, wg, ret, wo, out):
             nc.scalar.activation(out=silu[:], in_=g_bank[:], func=ACT.Silu)
             silus[j, c] = silu
 
-        h_operands = {}
+        h_tiles, h_operands = {}, {}
 
-        def quantise_h(j):
+        def gate_product(j):
             h_sb = work.tile([P, V], BF16)
             for h in range(HEADS):
                 cols = slice(h * HEAD_DIM, (h + 1) * HEAD_DIM)
@@ -193,7 +204,10 @@ def tile_retnet_pc_kernel(tc, x, wg, ret, wo, out):
                     op0=ALU.mult,
                     op1=ALU.mult,
                 )
-            h_words = h_sb[:].bitcast(F32)
+            h_tiles[j] = h_sb
+
+        def quantise_h(j):
+            h_words = h_tiles[j][:].bitcast(F32)
             h_grouped = pairs.tile([P, V], BF16, align_bytes=64)
             h_grouped_words = h_grouped[:].bitcast(F32)
             for b in range(2):
@@ -207,58 +221,80 @@ def tile_retnet_pc_kernel(tc, x, wg, ret, wo, out):
                     ),
                     in_=h_t[:].rearrange("p (c u s) -> p c s u", c=2, u=2),
                 )
-            h_codes = work.tile([P, V_PASSES * P], U32, align_bytes=64)
-            h_scales = work.tile([P, V_PASSES * P], U8, align_bytes=64)
+            h_codes = h_ops.tile([P, V_PASSES * P], U32, align_bytes=64)
+            h_scales = h_ops.tile([P, V_PASSES * P], U8, align_bytes=64)
             nc.vector.quantize_mx(out=h_codes[:].bitcast(FP8X4), scales=h_scales[:], in_=h_grouped[:])
             h_operands[j] = (h_codes, h_scales)
 
-        def project(j):
+        def project(j, n):
             h_codes, h_scales = h_operands[j]
-            for n in range(E_CHUNKS):
-                o_bank = o_banks.tile([P, N_TILE], F32)
-                for c in range(V_PASSES):
-                    nc.tensor.matmul_mx(
-                        out=o_bank[:],
-                        lhsT=h_codes[:, c * P : (c + 1) * P].bitcast(FP8X4),
-                        lhsT_scale=h_scales[:, c * P : (c + 1) * P],
-                        rhs=wo_codes[:, c, n * N_TILE : (n + 1) * N_TILE].bitcast(FP8X4),
-                        rhs_scale=wo_scales[:, c, n * N_TILE : (n + 1) * N_TILE],
-                        start=(c == 0),
-                        stop=(c == V_PASSES - 1),
-                    )
-                out_sb = store.tile([P, N_TILE], F32)
-                if n % 2 == 0:
-                    nc.vector.tensor_copy(out=out_sb[:], in_=o_bank[:])
-                else:
-                    nc.scalar.copy(out=out_sb[:], in_=o_bank[:])
-                nc.sync.dma_start(
-                    out=out_rows[j * P : (j + 1) * P, n * N_TILE : (n + 1) * N_TILE], in_=out_sb[:]
+            o_bank = o_banks.tile([P, N_TILE], F32)
+            for c in range(V_PASSES):
+                nc.tensor.matmul_mx(
+                    out=o_bank[:],
+                    lhsT=h_codes[:, c * P : (c + 1) * P].bitcast(FP8X4),
+                    lhsT_scale=h_scales[:, c * P : (c + 1) * P],
+                    rhs=wo_codes[:, c, n * N_TILE : (n + 1) * N_TILE].bitcast(FP8X4),
+                    rhs_scale=wo_scales[:, c, n * N_TILE : (n + 1) * N_TILE],
+                    start=(c == 0),
+                    stop=(c == V_PASSES - 1),
                 )
+            out_sb = store.tile([P, N_TILE], F32)
+            if n % 2 == 0 and j < FIRST_GROUP:
+                nc.vector.tensor_copy(out=out_sb[:], in_=o_bank[:])
+            else:
+                nc.scalar.copy(out=out_sb[:], in_=o_bank[:])
+            nc.sync.dma_start(
+                out=out_rows[j * P : (j + 1) * P, n * N_TILE : (n + 1) * N_TILE], in_=out_sb[:]
+            )
 
-        for j in range(FIRST_GROUP):
-            load_x(j)
-        for c in range(V_CHUNKS):
-            load_wg(c)
-            load_ret(c)
-
-        for j in range(FIRST_GROUP):
-            quantise_x(j)
-        for c in range(V_CHUNKS):
-            quantise_wg(c)
-            load_wo(c)
-            load_x(FIRST_GROUP + c)
-            load_ret(FIRST_GROUP + c)
+        with tc.manual_schedule():
+            load_wg(0)
             for j in range(FIRST_GROUP):
-                gate_chunk(j, c)
-            head_norms(c)
-        for c in range(V_PASSES):
-            quantise_wo(c)
-        for j in range(S_TILES):
-            quantise_h(j)
-            later = j + FIRST_GROUP
-            if later < S_TILES:
-                quantise_x(later)
-                head_norms(later)
-                for c in range(V_CHUNKS):
-                    gate_chunk(later, c)
-            project(j)
+                load_x(j)
+            load_wg(1)
+            load_ret(0)
+            load_wg(2)
+            load_ret(1)
+            load_wg(3)
+
+            for c in range(V_CHUNKS):
+                quantise_wg(c)
+                if c == 0:
+                    for j in range(FIRST_GROUP):
+                        quantise_x(j)
+                for j in range(FIRST_GROUP):
+                    gate_chunk(j, c)
+                if c < NORMS_AHEAD:
+                    head_norms(c)
+
+            load_wo(0)
+            load_wo(1)
+            load_ret(2)
+            load_ret(3)
+            load_x(4)
+            load_wo(2)
+            load_wo(3)
+            for j in range(5, S_TILES):
+                load_x(j)
+                load_ret(j - 1)
+            load_ret(S_TILES - 1)
+
+            for j in range(S_TILES + PROJECT_LAG):
+                if j < WO_STEPS:
+                    n, half = divmod(j, 2)
+                    quantise_wo(n, range(2 * half, 2 * half + 2))
+                if j >= PROJECT_LAG:
+                    for n in range(E_CHUNKS):
+                        project(j - PROJECT_LAG, n)
+                if j < S_TILES:
+                    gate_product(j)
+                if j + FIRST_GROUP < S_TILES:
+                    quantise_x(j + FIRST_GROUP)
+                if 1 <= j <= S_TILES:
+                    quantise_h(j - 1)
+                if j + NORMS_AHEAD < S_TILES:
+                    head_norms(j + NORMS_AHEAD)
+                if j + FIRST_GROUP < S_TILES:
+                    for c in range(V_CHUNKS):
+                        gate_chunk(j + FIRST_GROUP, c)

@@ -42,7 +42,6 @@ def tile_retnet_pc_kernel(tc, x, wg, ret, wo, out):
     x_rows = x.flatten_outer_dims()
     ret_rows = ret.rearrange("b s h d -> (b s) (h d)")
     out_rows = out.flatten_outer_dims()
-    wg_by_parity = wg.rearrange("(a q e) v -> e q a v", a=2 * E_PASSES, q=P, e=2)
 
     with (
         tc.tile_pool(name="const", bufs=1) as const,
@@ -89,10 +88,12 @@ def tile_retnet_pc_kernel(tc, x, wg, ret, wo, out):
         def load_wg(c):
             w_raw = w_in.tile([P, E_PASSES * PACK * N_TILE], BF16)
             planes = w_raw[:].rearrange("p (a e v) -> p a e v", a=2 * E_PASSES, e=2)
-            for e in range(2):
+            for a in range(2 * E_PASSES):
                 nc.sync.dma_start(
-                    out=planes[:, :, e, :],
-                    in_=wg_by_parity[e, :, :, c * N_TILE : (c + 1) * N_TILE],
+                    out=planes[:, a, :, :],
+                    in_=wg[a * 2 * P : (a + 1) * 2 * P, c * N_TILE : (c + 1) * N_TILE].rearrange(
+                        "(q e) v -> q e v", e=2
+                    ),
                 )
             wg_raws[c] = w_raw
 
@@ -215,7 +216,8 @@ def tile_retnet_pc_kernel(tc, x, wg, ret, wo, out):
                 for a in range(4):
                     w0 = (4 * b + a) * P
                     nc.tensor.transpose(h_t[:, a * P : (a + 1) * P], h_words[:, w0 : w0 + P], ident[:])
-                nc.scalar.copy(
+                copy_out = nc.scalar.copy if b == 0 else nc.vector.tensor_copy
+                copy_out(
                     out=h_grouped_words[:, b * N_TILE : (b + 1) * N_TILE].rearrange(
                         "p (c s u) -> p c s u", c=2, u=2
                     ),
@@ -249,15 +251,17 @@ def tile_retnet_pc_kernel(tc, x, wg, ret, wo, out):
             )
 
         with tc.manual_schedule():
+            load_ret(0)
+            load_x(0)
             load_wg(0)
-            for j in range(FIRST_GROUP):
+            for j in range(1, FIRST_GROUP):
                 load_x(j)
             load_wg(1)
-            load_ret(0)
-            load_wg(2)
             load_ret(1)
+            load_wg(2)
             load_wg(3)
 
+            head_norms(0)
             for c in range(V_CHUNKS):
                 quantise_wg(c)
                 if c == 0:
@@ -265,8 +269,8 @@ def tile_retnet_pc_kernel(tc, x, wg, ret, wo, out):
                         quantise_x(j)
                 for j in range(FIRST_GROUP):
                     gate_chunk(j, c)
-                if c < NORMS_AHEAD:
-                    head_norms(c)
+                if 1 <= c + 1 < NORMS_AHEAD:
+                    head_norms(c + 1)
 
             load_wo(0)
             load_wo(1)

@@ -5,6 +5,7 @@ F32 = mybir.dt.float32
 BF16 = mybir.dt.bfloat16
 U32 = mybir.dt.uint32
 U8 = mybir.dt.uint8
+I32 = mybir.dt.int32
 FP8X4 = mybir.dt.float8_e4m3fn_x4
 ACT = mybir.ActivationFunctionType
 ALU = mybir.AluOpType
@@ -24,7 +25,9 @@ E_CHUNKS = E // N_TILE
 HEADS_PER_CHUNK = N_TILE // HEAD_DIM
 FIRST_GROUP = 4
 WO_STEPS = 4
-NORMS_AHEAD = 2
+SQUARES_AHEAD = 3
+PAIR = 2
+RSQRT_GUESS = 0x5F3759DF - (1 << 22)
 PROJECT_LAG = 3
 assert PROJECT_LAG >= WO_STEPS - 1
 FLOPS = 2 * S * E * V + 2 * S * V * E
@@ -62,8 +65,6 @@ def tile_retnet_pc_kernel(tc, x, wg, ret, wo, out):
     ):
         ident = const.tile([P, P], F32)
         make_identity(nc, ident[:])
-        minus_half = const.tile([P, HEADS], F32)
-        nc.vector.memset(minus_half[:], -0.5)
         squares = const.tile([P, V], BF16)
 
         x_codes = keep.tile([P, S_TILES, E_PASSES * P], U32, align_bytes=64)
@@ -130,6 +131,7 @@ def tile_retnet_pc_kernel(tc, x, wg, ret, wo, out):
             for g in range(E_PASSES):
                 grouped = group.tile([P, PACK * N_TILE], BF16, align_bytes=64)
                 regroup(nc.vector.tensor_copy, grouped[:], planes[:, g])
+                next_small_step()
                 groupeds.append(grouped)
             for g in range(E_PASSES):
                 nc.vector.quantize_mx(
@@ -137,6 +139,7 @@ def tile_retnet_pc_kernel(tc, x, wg, ret, wo, out):
                     scales=wg_scales[:, g, cols],
                     in_=groupeds[g][:],
                 )
+                next_small_step()
 
         def quantise_wo(n, passes):
             cols = slice(n * N_TILE, (n + 1) * N_TILE)
@@ -145,6 +148,7 @@ def tile_retnet_pc_kernel(tc, x, wg, ret, wo, out):
                 planes = wo_raws[c][:].rearrange("p (t n) -> p t n", t=PACK)
                 grouped = group.tile([P, PACK * N_TILE], BF16, align_bytes=64)
                 regroup(nc.vector.tensor_copy, grouped[:], planes[:, :, cols])
+                next_small_step()
                 groupeds[c] = grouped
             for c in passes:
                 nc.vector.quantize_mx(
@@ -152,27 +156,74 @@ def tile_retnet_pc_kernel(tc, x, wg, ret, wo, out):
                     scales=wo_scales[:, c, cols],
                     in_=groupeds[c][:],
                 )
+                next_small_step()
 
-        rstds, silus = {}, {}
+        sumsqs, rstds, silus = {}, {}, {}
+        small_steps = []
 
-        def head_norms(j):
-            sumsq = stats.tile([P, HEADS], F32)
+        def next_small_step():
+            if small_steps:
+                small_steps.pop(0)()
+
+        def square_sums(j):
+            if j % PAIR == 0:
+                sumsq_pair = stats.tile([P, PAIR * HEADS], F32)
+                sumsqs[j // PAIR] = sumsq_pair
+            sumsq = sumsqs[j // PAIR]
             for h in range(HEADS):
                 cols = slice(h * HEAD_DIM, (h + 1) * HEAD_DIM)
+                column = (j % PAIR) * HEADS + h
                 nc.scalar.activation(
                     out=squares[:, cols],
                     in_=ret_tiles[j][:, cols],
                     func=ACT.Square,
-                    accum_out=sumsq[:, h : h + 1],
+                    accum_out=sumsq[:, column : column + 1],
                 )
-            meansq = stats.tile([P, HEADS], F32)
-            nc.gpsimd.tensor_scalar(
-                out=meansq[:], in0=sumsq[:], scalar1=1.0 / HEAD_DIM, scalar2=EPS,
-                op0=ALU.mult, op1=ALU.add,
-            )
-            rstd = stats.tile([P, HEADS], F32)
-            nc.gpsimd.tensor_tensor(out=rstd[:], in0=meansq[:], in1=minus_half[:], op=ALU.pow)
-            rstds[j] = rstd
+
+        def queue_rstd(pair):
+            sumsq = sumsqs[pair]
+            half = stats.tile([P, PAIR * HEADS], F32)
+            shifted = stats.tile([P, PAIR * HEADS], I32)
+            root = stats.tile([P, PAIR * HEADS], I32)
+            root_square = stats.tile([P, PAIR * HEADS], F32)
+            rest = stats.tile([P, PAIR * HEADS], F32)
+            y = root[:].bitcast(F32)
+
+            def halve():
+                nc.vector.tensor_scalar(
+                    out=half[:], in0=sumsq[:], scalar1=0.5 / HEAD_DIM, scalar2=0.5 * EPS,
+                    op0=ALU.mult, op1=ALU.add,
+                )
+
+            def shift():
+                nc.vector.tensor_scalar(
+                    out=shifted[:], in0=half[:].bitcast(I32), scalar1=1, scalar2=None,
+                    op0=ALU.logical_shift_right,
+                )
+
+            def guess():
+                nc.vector.tensor_scalar(
+                    out=root[:], in0=shifted[:], scalar1=-1.0, scalar2=float(RSQRT_GUESS),
+                    op0=ALU.mult, op1=ALU.add,
+                )
+
+            def square():
+                nc.vector.tensor_tensor(out=root_square[:], in0=y, in1=y, op=ALU.mult)
+
+            def negate():
+                nc.vector.scalar_tensor_tensor(
+                    out=rest[:], in0=root_square[:], scalar=-1.0, in1=half[:],
+                    op0=ALU.mult, op1=ALU.mult,
+                )
+
+            def improve():
+                nc.vector.scalar_tensor_tensor(
+                    out=y, in0=rest[:], scalar=1.5, in1=y, op0=ALU.add, op1=ALU.mult
+                )
+
+            small_steps.extend([halve, shift, guess] + 3 * [square, negate, improve])
+            for i in range(PAIR):
+                rstds[PAIR * pair + i] = y[:, i * HEADS : (i + 1) * HEADS]
 
         def gate_chunk(j, c):
             g_bank = g_banks.tile([P, N_TILE], F32)
@@ -205,6 +256,7 @@ def tile_retnet_pc_kernel(tc, x, wg, ret, wo, out):
                     op0=ALU.mult,
                     op1=ALU.mult,
                 )
+                next_small_step()
             h_tiles[j] = h_sb
 
         def quantise_h(j):
@@ -259,9 +311,10 @@ def tile_retnet_pc_kernel(tc, x, wg, ret, wo, out):
             load_wg(1)
             load_ret(1)
             load_wg(2)
+            load_ret(2)
             load_wg(3)
 
-            head_norms(0)
+            square_sums(0)
             for c in range(V_CHUNKS):
                 quantise_wg(c)
                 if c == 0:
@@ -269,12 +322,13 @@ def tile_retnet_pc_kernel(tc, x, wg, ret, wo, out):
                         quantise_x(j)
                 for j in range(FIRST_GROUP):
                     gate_chunk(j, c)
-                if 1 <= c + 1 < NORMS_AHEAD:
-                    head_norms(c + 1)
+                if c + 1 < SQUARES_AHEAD:
+                    square_sums(c + 1)
+                if c == 1:
+                    queue_rstd(0)
 
             load_wo(0)
             load_wo(1)
-            load_ret(2)
             load_ret(3)
             load_x(4)
             load_wo(2)
@@ -291,14 +345,18 @@ def tile_retnet_pc_kernel(tc, x, wg, ret, wo, out):
                 if j >= PROJECT_LAG:
                     for n in range(E_CHUNKS):
                         project(j - PROJECT_LAG, n)
+                if j % PAIR == 1 and j + 1 < S_TILES:
+                    queue_rstd((j + 1) // PAIR)
                 if j < S_TILES:
                     gate_product(j)
                 if j + FIRST_GROUP < S_TILES:
                     quantise_x(j + FIRST_GROUP)
                 if 1 <= j <= S_TILES:
                     quantise_h(j - 1)
-                if j + NORMS_AHEAD < S_TILES:
-                    head_norms(j + NORMS_AHEAD)
+                while small_steps:
+                    next_small_step()
+                if j + SQUARES_AHEAD < S_TILES:
+                    square_sums(j + SQUARES_AHEAD)
                 if j + FIRST_GROUP < S_TILES:
                     for c in range(V_CHUNKS):
                         gate_chunk(j + FIRST_GROUP, c)

@@ -23,13 +23,8 @@ V_PASSES = V // K_PASS
 V_CHUNKS = V // N_TILE
 E_CHUNKS = E // N_TILE
 HEADS_PER_CHUNK = N_TILE // HEAD_DIM
-FIRST_GROUP = 4
-WO_STEPS = 4
-SQUARES_AHEAD = 3
-PAIR = 2
+BATCHES = ((0, 1), (2, 3), (4, 5), (6, 7))
 RSQRT_GUESS = 0x5F3759DF - (1 << 22)
-PROJECT_LAG = 3
-assert PROJECT_LAG >= WO_STEPS - 1
 FLOPS = 2 * S * E * V + 2 * S * V * E
 
 
@@ -48,16 +43,17 @@ def tile_retnet_pc_kernel(tc, x, wg, ret, wo, out):
 
     with (
         tc.tile_pool(name="const", bufs=1) as const,
-        tc.tile_pool(name="x_in", bufs=S_TILES) as x_in,
+        tc.tile_pool(name="x_in", bufs=6) as x_in,
         tc.tile_pool(name="ret_in", bufs=S_TILES) as ret_in,
-        tc.tile_pool(name="w_in", bufs=4) as w_in,
+        tc.tile_pool(name="w_in", bufs=8) as w_in,
         tc.tile_pool(name="keep", bufs=1) as keep,
         tc.tile_pool(name="group", bufs=3) as group,
-        tc.tile_pool(name="gate", bufs=18) as gate,
-        tc.tile_pool(name="stats", bufs=S_TILES) as stats,
-        tc.tile_pool(name="pairs", bufs=3) as pairs,
+        tc.tile_pool(name="gate", bufs=24) as gate,
+        tc.tile_pool(name="stats", bufs=2) as stats,
+        tc.tile_pool(name="x_pairs", bufs=3) as x_pairs,
+        tc.tile_pool(name="h_pairs", bufs=2) as h_pairs,
         tc.tile_pool(name="work", bufs=2) as work,
-        tc.tile_pool(name="h_ops", bufs=5) as h_ops,
+        tc.tile_pool(name="h_ops", bufs=6) as h_ops,
         tc.tile_pool(name="store", bufs=4) as store,
         tc.psum_pool(name="g_banks", bufs=4) as g_banks,
         tc.psum_pool(name="t_banks", bufs=2) as t_banks,
@@ -73,146 +69,119 @@ def tile_retnet_pc_kernel(tc, x, wg, ret, wo, out):
         wg_scales = keep.tile([P, E_PASSES, V], U8, align_bytes=64)
         wo_codes = keep.tile([P, V_PASSES, E], U32, align_bytes=64)
         wo_scales = keep.tile([P, V_PASSES, E], U8, align_bytes=64)
+        weights = {"g": (wg, wg_codes, wg_scales), "o": (wo, wo_codes, wo_scales)}
 
-        x_tiles, ret_tiles, wg_raws, wo_raws = {}, {}, {}, {}
+        made = {}
+        taken = {"g": 0, "t": 0, "o": 0}
+        banks = {"g": 4, "t": 2, "o": 2}
 
         def load_x(j):
             x_sb = x_in.tile([P, E], BF16)
             nc.sync.dma_start(out=x_sb[:], in_=x_rows[j * P : (j + 1) * P, :])
-            x_tiles[j] = x_sb
+            made["x", j] = x_sb
 
         def load_ret(j):
             ret_sb = ret_in.tile([P, V], BF16)
             nc.sync.dma_start(out=ret_sb[:], in_=ret_rows[j * P : (j + 1) * P, :])
-            ret_tiles[j] = ret_sb
+            made["ret", j] = ret_sb
 
-        def load_wg(c):
-            w_raw = w_in.tile([P, E_PASSES * PACK * N_TILE], BF16)
-            planes = w_raw[:].rearrange("p (a e v) -> p a e v", a=2 * E_PASSES, e=2)
-            for a in range(2 * E_PASSES):
-                nc.sync.dma_start(
-                    out=planes[:, a, :, :],
-                    in_=wg[a * 2 * P : (a + 1) * 2 * P, c * N_TILE : (c + 1) * N_TILE].rearrange(
-                        "(q e) v -> q e v", e=2
-                    ),
-                )
-            wg_raws[c] = w_raw
+        def load_w(w, n, c):
+            w_raw = w_in.tile([P, PACK * N_TILE], BF16)
+            planes = w_raw[:].rearrange("p (u e v) -> p u e v", u=2, e=2)
+            rows = weights[w][0][c * K_PASS : (c + 1) * K_PASS, n * N_TILE : (n + 1) * N_TILE]
+            rows = rows.rearrange("(u q e) v -> u q e v", u=2, e=2)
+            for u in range(2):
+                nc.sync.dma_start(out=planes[:, u, :, :], in_=rows[u])
+            made["raw", w, n, c] = w_raw
 
-        def load_wo(c):
-            w_raw = w_in.tile([P, PACK * E], BF16)
-            nc.sync.dma_start(
-                out=w_raw[:].rearrange("p (u r) -> p u r", u=2),
-                in_=wo[c * K_PASS : (c + 1) * K_PASS, :].rearrange(
-                    "(u q e) n -> q u (e n)", u=2, q=P, e=2
-                ),
-            )
-            wo_raws[c] = w_raw
-
-        def quantise_x(j):
-            x_words = x_tiles[j][:].bitcast(F32)
+        def turn_x(j):
+            x_words = made["x", j][:].bitcast(F32)
             x_t = t_banks.tile([P, N_TILE], F32, tag="t_bank")
             for a in range(2 * E_PASSES):
                 nc.tensor.transpose(
                     x_t[:, a * P : (a + 1) * P], x_words[:, a * P : (a + 1) * P], ident[:]
                 )
-            x_grouped = pairs.tile([P, E], BF16, align_bytes=64)
-            nc.scalar.copy(
+            made["x_t", j] = x_t
+            taken["t"] += 1
+
+        def copy_x(j, copy):
+            x_grouped = x_pairs.tile([P, E], BF16, align_bytes=64)
+            copy(
                 out=x_grouped[:].bitcast(F32).rearrange("p (g s u) -> p g s u", g=E_PASSES, u=2),
-                in_=x_t[:].rearrange("p (g u s) -> p g s u", g=E_PASSES, u=2),
+                in_=made["x_t", j][:].rearrange("p (g u s) -> p g s u", g=E_PASSES, u=2),
             )
+            made["x_grouped", j] = x_grouped
+            taken["t"] -= 1
+
+        def quantise_x(j):
             nc.vector.quantize_mx(
-                out=x_codes[:, j, :].bitcast(FP8X4), scales=x_scales[:, j, :], in_=x_grouped[:]
+                out=x_codes[:, j, :].bitcast(FP8X4), scales=x_scales[:, j, :],
+                in_=made["x_grouped", j][:],
             )
+            made["xq", j] = True
+            next_small(1)
 
-        def quantise_wg(c):
-            planes = wg_raws[c][:].rearrange("p (g t v) -> p g t v", g=E_PASSES, t=PACK)
-            cols = slice(c * N_TILE, (c + 1) * N_TILE)
-            groupeds = []
-            for g in range(E_PASSES):
-                grouped = group.tile([P, PACK * N_TILE], BF16, align_bytes=64)
-                regroup(nc.vector.tensor_copy, grouped[:], planes[:, g])
-                next_small_step()
-                groupeds.append(grouped)
-            for g in range(E_PASSES):
-                nc.vector.quantize_mx(
-                    out=wg_codes[:, g, cols].bitcast(FP8X4),
-                    scales=wg_scales[:, g, cols],
-                    in_=groupeds[g][:],
-                )
-                next_small_step()
+        def group_w(w, n, c):
+            grouped = group.tile([P, PACK * N_TILE], BF16, align_bytes=64)
+            planes = made["raw", w, n, c][:].rearrange("p (t v) -> p t v", t=PACK)
+            regroup(nc.vector.tensor_copy, grouped[:], planes)
+            made["grouped", w, n, c] = grouped
+            next_small(1)
 
-        def quantise_wo(n, passes):
+        def quantise_w(w, n, c):
             cols = slice(n * N_TILE, (n + 1) * N_TILE)
-            groupeds = {}
-            for c in passes:
-                planes = wo_raws[c][:].rearrange("p (t n) -> p t n", t=PACK)
-                grouped = group.tile([P, PACK * N_TILE], BF16, align_bytes=64)
-                regroup(nc.vector.tensor_copy, grouped[:], planes[:, :, cols])
-                next_small_step()
-                groupeds[c] = grouped
-            for c in passes:
-                nc.vector.quantize_mx(
-                    out=wo_codes[:, c, cols].bitcast(FP8X4),
-                    scales=wo_scales[:, c, cols],
-                    in_=groupeds[c][:],
-                )
-                next_small_step()
+            nc.vector.quantize_mx(
+                out=weights[w][1][:, c, cols].bitcast(FP8X4),
+                scales=weights[w][2][:, c, cols],
+                in_=made["grouped", w, n, c][:],
+            )
+            made["wq", w, n, c] = True
+            next_small(1)
 
-        sumsqs, rstds, silus = {}, {}, {}
-        small_steps = []
-
-        def next_small_step():
-            if small_steps:
-                small_steps.pop(0)()
-
-        def square_sums(j):
-            if j % PAIR == 0:
-                sumsq_pair = stats.tile([P, PAIR * HEADS], F32)
-                sumsqs[j // PAIR] = sumsq_pair
-            sumsq = sumsqs[j // PAIR]
-            for h in range(HEADS):
+        def sum_squares(j, first, last):
+            if ("sumsq", j) not in made:
+                b = [j in batch for batch in BATCHES].index(True)
+                sumsq = stats.tile([P, len(BATCHES[b]) * HEADS], F32)
+                made["sumsq_all", b] = sumsq
+                for i, tile in enumerate(BATCHES[b]):
+                    made["sumsq", tile] = sumsq[:, i * HEADS : (i + 1) * HEADS]
+            for h in range(first, last):
                 cols = slice(h * HEAD_DIM, (h + 1) * HEAD_DIM)
-                column = (j % PAIR) * HEADS + h
                 nc.scalar.activation(
                     out=squares[:, cols],
-                    in_=ret_tiles[j][:, cols],
+                    in_=made["ret", j][:, cols],
                     func=ACT.Square,
-                    accum_out=sumsq[:, column : column + 1],
+                    accum_out=made["sumsq", j][:, h : h + 1],
                 )
+            if last == HEADS:
+                made["sq", j] = True
 
-        def queue_rstd(pair):
-            sumsq = sumsqs[pair]
-            half = stats.tile([P, PAIR * HEADS], F32)
-            shifted = stats.tile([P, PAIR * HEADS], I32)
-            root = stats.tile([P, PAIR * HEADS], I32)
-            root_square = stats.tile([P, PAIR * HEADS], F32)
-            rest = stats.tile([P, PAIR * HEADS], F32)
-            y = root[:].bitcast(F32)
+        def root(b):
+            width = len(BATCHES[b]) * HEADS
+            half = stats.tile([P, width], F32)
+            rstd = stats.tile([P, width], I32)
+            square = stats.tile([P, width], F32)
+            rest = stats.tile([P, width], F32)
+            y = rstd[:].bitcast(F32)
 
-            def halve():
+            def first():
                 nc.vector.tensor_scalar(
-                    out=half[:], in0=sumsq[:], scalar1=0.5 / HEAD_DIM, scalar2=0.5 * EPS,
-                    op0=ALU.mult, op1=ALU.add,
-                )
-
-            def shift():
-                nc.vector.tensor_scalar(
-                    out=shifted[:], in0=half[:].bitcast(I32), scalar1=1, scalar2=None,
-                    op0=ALU.logical_shift_right,
+                    out=half[:], in0=made["sumsq_all", b][:], scalar1=0.5 / HEAD_DIM,
+                    scalar2=0.5 * EPS, op0=ALU.mult, op1=ALU.add,
                 )
 
             def guess():
                 nc.vector.tensor_scalar(
-                    out=root[:], in0=shifted[:], scalar1=-1.0, scalar2=float(RSQRT_GUESS),
+                    out=rstd[:], in0=half[:].bitcast(I32), scalar1=-0.5, scalar2=float(RSQRT_GUESS),
                     op0=ALU.mult, op1=ALU.add,
                 )
 
-            def square():
-                nc.vector.tensor_tensor(out=root_square[:], in0=y, in1=y, op=ALU.mult)
+            def multiply():
+                nc.vector.tensor_tensor(out=square[:], in0=y, in1=y, op=ALU.mult)
 
             def negate():
                 nc.vector.scalar_tensor_tensor(
-                    out=rest[:], in0=root_square[:], scalar=-1.0, in1=half[:],
+                    out=rest[:], in0=square[:], scalar=-1.0, in1=half[:],
                     op0=ALU.mult, op1=ALU.mult,
                 )
 
@@ -221,11 +190,22 @@ def tile_retnet_pc_kernel(tc, x, wg, ret, wo, out):
                     out=y, in0=rest[:], scalar=1.5, in1=y, op0=ALU.add, op1=ALU.mult
                 )
 
-            small_steps.extend([halve, shift, guess] + 3 * [square, negate, improve])
-            for i in range(PAIR):
-                rstds[PAIR * pair + i] = y[:, i * HEADS : (i + 1) * HEADS]
+            small.extend([first, guess] + 3 * [multiply, negate, improve])
+            made["roots", b] = y
 
-        def gate_chunk(j, c):
+        small = []
+
+        def next_small(count):
+            for i in range(count):
+                if small:
+                    small.pop(0)()
+
+        def finish_root(b):
+            next_small(len(small))
+            for i, j in enumerate(BATCHES[b]):
+                made["rstd", j] = made["roots", b][:, i * HEADS : (i + 1) * HEADS]
+
+        def gate_product(j, c):
             g_bank = g_banks.tile([P, N_TILE], F32)
             for g in range(E_PASSES):
                 nc.tensor.matmul_mx(
@@ -237,126 +217,168 @@ def tile_retnet_pc_kernel(tc, x, wg, ret, wo, out):
                     start=(g == 0),
                     stop=(g == E_PASSES - 1),
                 )
-            silu = gate.tile([P, N_TILE], F32)
-            nc.scalar.activation(out=silu[:], in_=g_bank[:], func=ACT.Silu)
-            silus[j, c] = silu
+            made["g", j, c] = g_bank
+            taken["g"] += 1
 
-        h_tiles, h_operands = {}, {}
+        def silu(j, c):
+            silu_sb = gate.tile([P, N_TILE], F32)
+            nc.scalar.activation(out=silu_sb[:], in_=made["g", j, c][:], func=ACT.Silu)
+            made["silu", j, c] = silu_sb
+            taken["g"] -= 1
 
-        def gate_product(j):
-            h_sb = work.tile([P, V], BF16)
-            for h in range(HEADS):
+        def form_h(j, first, last):
+            if first == 0:
+                h_sb = work.tile([P, V], BF16)
+                made["h", j] = h_sb
+            for h in range(first, last):
                 cols = slice(h * HEAD_DIM, (h + 1) * HEAD_DIM)
                 part = slice((h % HEADS_PER_CHUNK) * HEAD_DIM, (h % HEADS_PER_CHUNK + 1) * HEAD_DIM)
                 nc.vector.scalar_tensor_tensor(
-                    out=h_sb[:, cols],
-                    in0=silus[j, h // HEADS_PER_CHUNK][:, part],
-                    scalar=rstds[j][:, h : h + 1],
-                    in1=ret_tiles[j][:, cols],
+                    out=made["h", j][:, cols],
+                    in0=made["silu", j, h // HEADS_PER_CHUNK][:, part],
+                    scalar=made["rstd", j][:, h : h + 1],
+                    in1=made["ret", j][:, cols],
                     op0=ALU.mult,
                     op1=ALU.mult,
                 )
-                next_small_step()
-            h_tiles[j] = h_sb
+                next_small(1)
+            made["h_half", j, last // 4 - 1] = True
+            if last - first == HEADS:
+                made["h_half", j, 0] = True
 
-        def quantise_h(j):
-            h_words = h_tiles[j][:].bitcast(F32)
-            h_grouped = pairs.tile([P, V], BF16, align_bytes=64)
-            h_grouped_words = h_grouped[:].bitcast(F32)
-            for b in range(2):
-                h_t = t_banks.tile([P, N_TILE], F32, tag="t_bank")
-                for a in range(4):
-                    w0 = (4 * b + a) * P
-                    nc.tensor.transpose(h_t[:, a * P : (a + 1) * P], h_words[:, w0 : w0 + P], ident[:])
-                copy_out = nc.scalar.copy if b == 0 else nc.vector.tensor_copy
-                copy_out(
-                    out=h_grouped_words[:, b * N_TILE : (b + 1) * N_TILE].rearrange(
-                        "p (c s u) -> p c s u", c=2, u=2
-                    ),
-                    in_=h_t[:].rearrange("p (c u s) -> p c s u", c=2, u=2),
-                )
-            h_codes = h_ops.tile([P, V_PASSES * P], U32, align_bytes=64)
-            h_scales = h_ops.tile([P, V_PASSES * P], U8, align_bytes=64)
-            nc.vector.quantize_mx(out=h_codes[:].bitcast(FP8X4), scales=h_scales[:], in_=h_grouped[:])
-            h_operands[j] = (h_codes, h_scales)
+        def turn_h(j, b):
+            h_words = made["h", j][:].bitcast(F32)
+            h_t = t_banks.tile([P, N_TILE], F32, tag="t_bank")
+            for a in range(4):
+                w0 = (4 * b + a) * P
+                nc.tensor.transpose(h_t[:, a * P : (a + 1) * P], h_words[:, w0 : w0 + P], ident[:])
+            made["h_t", j, b] = h_t
+            taken["t"] += 1
 
-        def project(j, n):
-            h_codes, h_scales = h_operands[j]
-            o_bank = o_banks.tile([P, N_TILE], F32)
-            for c in range(V_PASSES):
+        def copy_h(j, b, copy):
+            if ("h_grouped", j) not in made:
+                h_grouped = h_pairs.tile([P, V], BF16, align_bytes=64)
+                made["h_grouped", j] = h_grouped
+            copy(
+                out=made["h_grouped", j][:].bitcast(F32)[:, b * N_TILE : (b + 1) * N_TILE].rearrange(
+                    "p (c s u) -> p c s u", c=2, u=2
+                ),
+                in_=made["h_t", j, b][:].rearrange("p (c u s) -> p c s u", c=2, u=2),
+            )
+            made["h_copied", j, b] = True
+            taken["t"] -= 1
+
+        def quantise_h(j, halves):
+            if 0 in halves:
+                h_codes = h_ops.tile([P, V_PASSES * P], U32, align_bytes=64)
+                h_scales = h_ops.tile([P, V_PASSES * P], U8, align_bytes=64)
+                made["h_ops", j] = (h_codes, h_scales)
+            codes, scales = made["h_ops", j]
+            words = slice(halves[0] * 2 * P, (halves[-1] + 1) * 2 * P)
+            values = slice(halves[0] * V // 2, (halves[-1] + 1) * V // 2)
+            nc.vector.quantize_mx(
+                out=codes[:, words].bitcast(FP8X4), scales=scales[:, words],
+                in_=made["h_grouped", j][:, values],
+            )
+            for b in halves:
+                made["hq", j, b] = True
+            next_small(1)
+
+        def project(j, n, passes):
+            codes, scales = made["h_ops", j]
+            if passes[0] == 0:
+                o_bank = o_banks.tile([P, N_TILE], F32)
+                made["o_bank", j, n] = o_bank
+                taken["o"] += 1
+            for c in passes:
                 nc.tensor.matmul_mx(
-                    out=o_bank[:],
-                    lhsT=h_codes[:, c * P : (c + 1) * P].bitcast(FP8X4),
-                    lhsT_scale=h_scales[:, c * P : (c + 1) * P],
+                    out=made["o_bank", j, n][:],
+                    lhsT=codes[:, c * P : (c + 1) * P].bitcast(FP8X4),
+                    lhsT_scale=scales[:, c * P : (c + 1) * P],
                     rhs=wo_codes[:, c, n * N_TILE : (n + 1) * N_TILE].bitcast(FP8X4),
                     rhs_scale=wo_scales[:, c, n * N_TILE : (n + 1) * N_TILE],
                     start=(c == 0),
                     stop=(c == V_PASSES - 1),
                 )
+            if passes[-1] == V_PASSES - 1:
+                made["o", j, n] = True
+
+        def copy_out(j, n, copy):
             out_sb = store.tile([P, N_TILE], F32)
-            if n % 2 == 0 and j < FIRST_GROUP:
-                nc.vector.tensor_copy(out=out_sb[:], in_=o_bank[:])
-            else:
-                nc.scalar.copy(out=out_sb[:], in_=o_bank[:])
+            copy(out=out_sb[:], in_=made["o_bank", j, n][:])
             nc.sync.dma_start(
                 out=out_rows[j * P : (j + 1) * P, n * N_TILE : (n + 1) * N_TILE], in_=out_sb[:]
             )
+            taken["o"] -= 1
 
+        copies = {"V": nc.vector.tensor_copy, "S": nc.scalar.copy}
+
+        def LX(j): return ([], "", load_x, (j,))
+        def LR(j): return ([], "", load_ret, (j,))
+        def LW(w, n, c): return ([], "", load_w, (w, n, c))
+        def XT(j): return ([("x", j)], "t", turn_x, (j,))
+        def XE(j, e="S"): return ([("x_t", j)], "", copy_x, (j, copies[e]))
+        def XQ(j): return ([("x_grouped", j)], "", quantise_x, (j,))
+        def I(w, n, c): return ([("raw", w, n, c)], "", group_w, (w, n, c))
+        def Q(w, n, c): return ([("grouped", w, n, c)], "", quantise_w, (w, n, c))
+        def SQ(j, a=0, b=4): return [([("ret", j)], "", sum_squares, (j, 2 * a, 2 * b))]
+        def N(b): return ([("sq", j) for j in BATCHES[b]], "", root, (b,))
+        def NF(b): return ([("roots", b)], "", finish_root, (b,))
+        def G1(j, c): return ([("xq", j)] + [("wq", "g", c, g) for g in range(E_PASSES)], "g", gate_product, (j, c))
+        def SI1(j, c): return ([("g", j, c)], "", silu, (j, c))
+        def PR(j, a=0, b=HEADS): return ([("silu", j, c) for c in range(a // 2, b // 2)] + [("rstd", j), ("ret", j)], "", form_h, (j, a, b))
+        def HT1(j, b): return ([("h_half", j, b)], "t", turn_h, (j, b))
+        def HE1(j, b, e="S"): return ([("h_t", j, b)], "", copy_h, (j, b, copies[e]))
+        def HQ(j, halves=(0, 1)): return ([("h_copied", j, b) for b in halves], "", quantise_h, (j, halves))
+        def O1(j, n, passes=(0, 1, 2, 3)): return ([("hq", j, c // 2) for c in passes] + [("wq", "o", n, c) for c in passes], "o" if passes[0] == 0 else "", project, (j, n, passes))
+        def OE(e, *pairs): return [([("o", j, n)], "", copy_out, (j, n, copies[e])) for j, n in pairs]
+        def O(*pairs): return [O1(j, n) for j, n in pairs]
+        def W(w, n, cs): return [I(w, n, c) for c in cs] + [Q(w, n, c) for c in cs]
+        def SI(j): return [SI1(j, c) for c in four]
+        def G(j): return [G1(j, c) for c in four]
+        def HE(j, e="S"): return [HE1(j, 0, e), HE1(j, 1, e)]
+        def HT(j): return [HT1(j, 0), HT1(j, 1)]
+        def P2(j): return [PR(j, 0, 4), PR(j, 4, 8)]
+
+        def issue(programs):
+            while any(programs):
+                moved = False
+                for program in programs:
+                    if program:
+                        names, bank, step, arguments = program[0]
+                        if all([name in made for name in names]) and (not bank or taken[bank] < banks[bank]):
+                            step(*arguments)
+                            program.pop(0)
+                            moved = True
+                assert moved
+
+        four = range(4)
+        loads = [LW("g", 0, 0), LW("g", 0, 1), LX(0), LX(1), LR(0), LX(2), LX(3), LW("g", 1, 0), LW("g", 1, 1), LR(1), LW("g", 2, 0), LW("g", 2, 1), LX(4), LW("g", 3, 0), LW("g", 3, 1), LX(5), LR(2), LW("o", 0, 0), LW("o", 0, 1), LX(6), LW("o", 0, 2), LW("o", 0, 3), LR(3), LX(7), LW("o", 1, 0), LW("o", 1, 1), LR(4), LR(5), LW("o", 1, 2), LW("o", 1, 3), LR(6), LR(7)]
+        vector = W("g", 0, (0, 1)) + [XQ(0), XQ(1), I("g", 1, 0), XQ(2), XQ(3), I("g", 1, 1), Q("g", 1, 0), Q("g", 1, 1)]
+        vector += W("g", 2, (0, 1)) + [N(0)] + W("g", 3, (0, 1))
+        scalar = [XE(0), XE(1)] + SQ(0, 0, 2) + [XE(2), XE(3)] + SQ(0, 2, 4)
+        scalar += [SI1(j, 0) for j in four] + SQ(1) + [SI1(j, 1) for j in four] + [SI1(j, 2) for j in four] + [XE(4)] + SQ(2, 0, 2) + [SI1(j, 3) for j in four]
+        tensor = [XT(j) for j in four] + [G1(j, c) for c in (0, 1, 2) for j in four] + [XT(4)] + [G1(j, 3) for j in four] + [XT(5)]
+        slots = [
+            ([NF(0)] + P2(0) + [XQ(4)], [XE(5)] + SQ(2, 2, 4) + SI(4), G(4)),
+            (P2(1) + [XQ(5)], HE(0), HT(0) + G(5)),
+            (W("o", 0, (0, 1)) + [HQ(0)], HE(1) + SI(5) + [XE(6)], HT(1) + [XT(6)]),
+            (W("o", 0, (2, 3)) + [HQ(1), XQ(6)], SQ(3) + [XE(7)], O((0, 0)) + [XT(7)]),
+            (W("o", 1, (0, 1)) + [XQ(7)], OE("S", (0, 0)) + SI(6) + OE("S", (1, 0)), G(6) + O((1, 0))),
+            ([N(1)] + W("o", 1, (2, 3)), SQ(4) + SQ(5, 0, 2), []),
+            ([NF(1)] + P2(2), SI(7), G(7)),
+            ([PR(3, 0, 4)] + HE(2, "V") + [PR(3, 4, 8)], SQ(5, 2, 4) + OE("S", (0, 1)) + SQ(6), HT(2) + O((0, 1))),
+            ([HQ(2), N(2), NF(2)] + P2(4) + [HE1(3, 0, "V")], SQ(7) + OE("S", (1, 1)) + [HE1(3, 1)], O((1, 1)) + HT(3) + O((2, 0))),
+            ([N(3), HQ(3)] + P2(5), OE("S", (2, 0)) + HE(4) + OE("S", (2, 1)), HT(4) + O((2, 1), (3, 0))),
+            ([HQ(4), NF(3)] + P2(6), OE("S", (3, 0)) + HE(5) + OE("S", (3, 1)), O((3, 1)) + HT(5) + O((4, 0))),
+            ([HQ(5)] + P2(7), OE("S", (4, 0), (4, 1)) + HE(6), O((4, 1)) + HT(6) + O((5, 0))),
+            ([HQ(6)] + OE("V", (5, 1)), OE("S", (5, 0)) + HE(7), HT(7) + O((5, 1))),
+            ([HQ(7, (0,)), HQ(7, (1,))] + OE("V", (6, 1)), OE("S", (6, 0)), O((6, 0), (6, 1)) + [O1(7, 0, (0, 1)), O1(7, 0, (2, 3)), O1(7, 1, (0, 1)), O1(7, 1, (2, 3))]),
+            (OE("V", (7, 1)), OE("S", (7, 0)), []),
+        ]
+        for v, s, p in slots:
+            vector += v
+            scalar += s
+            tensor += p
         with tc.manual_schedule():
-            load_ret(0)
-            load_x(0)
-            load_wg(0)
-            for j in range(1, FIRST_GROUP):
-                load_x(j)
-            load_wg(1)
-            load_ret(1)
-            load_wg(2)
-            load_ret(2)
-            load_wg(3)
-
-            square_sums(0)
-            for c in range(V_CHUNKS):
-                quantise_wg(c)
-                if c == 0:
-                    for j in range(FIRST_GROUP):
-                        quantise_x(j)
-                for j in range(FIRST_GROUP):
-                    gate_chunk(j, c)
-                if c + 1 < SQUARES_AHEAD:
-                    square_sums(c + 1)
-                if c == 1:
-                    queue_rstd(0)
-
-            load_wo(0)
-            load_wo(1)
-            load_ret(3)
-            load_x(4)
-            load_wo(2)
-            load_wo(3)
-            for j in range(5, S_TILES):
-                load_x(j)
-                load_ret(j - 1)
-            load_ret(S_TILES - 1)
-
-            for j in range(S_TILES + PROJECT_LAG):
-                if j < WO_STEPS:
-                    n, half = divmod(j, 2)
-                    quantise_wo(n, range(2 * half, 2 * half + 2))
-                if j >= PROJECT_LAG:
-                    for n in range(E_CHUNKS):
-                        project(j - PROJECT_LAG, n)
-                if j % PAIR == 1 and j + 1 < S_TILES:
-                    queue_rstd((j + 1) // PAIR)
-                if j < S_TILES:
-                    gate_product(j)
-                if j + FIRST_GROUP < S_TILES:
-                    quantise_x(j + FIRST_GROUP)
-                if 1 <= j <= S_TILES:
-                    quantise_h(j - 1)
-                while small_steps:
-                    next_small_step()
-                if j + SQUARES_AHEAD < S_TILES:
-                    square_sums(j + SQUARES_AHEAD)
-                if j + FIRST_GROUP < S_TILES:
-                    for c in range(V_CHUNKS):
-                        gate_chunk(j + FIRST_GROUP, c)
+            issue([loads, vector, tensor, scalar])

@@ -23,7 +23,7 @@ V_PASSES = V // K_PASS
 V_CHUNKS = V // N_TILE
 E_CHUNKS = E // N_TILE
 HEADS_PER_CHUNK = N_TILE // HEAD_DIM
-BATCHES = ((0, 1), (2, 3), (4, 5), (6, 7))
+BATCHES = ((0, 1), (2, 3, 4), (5, 6, 7))
 RSQRT_GUESS = 0x5F3759DF - (1 << 22)
 FLOPS = 2 * S * E * V + 2 * S * V * E
 
@@ -54,13 +54,15 @@ def tile_retnet_pc_kernel(tc, x, wg, ret, wo, out):
         tc.tile_pool(name="h_pairs", bufs=2) as h_pairs,
         tc.tile_pool(name="work", bufs=2) as work,
         tc.tile_pool(name="h_ops", bufs=6) as h_ops,
-        tc.tile_pool(name="store", bufs=4) as store,
-        tc.psum_pool(name="g_banks", bufs=4) as g_banks,
+        tc.tile_pool(name="store", bufs=5) as store,
         tc.psum_pool(name="t_banks", bufs=2) as t_banks,
-        tc.psum_pool(name="o_banks", bufs=2) as o_banks,
+        tc.psum_pool(name="m_banks", bufs=6) as m_banks,
     ):
         ident = const.tile([P, P], F32)
         make_identity(nc, ident[:])
+        primer = const.tile([P, 1], F32)
+        nc.vector.memset(primer[:], 0.0)
+        nc.scalar.activation(out=primer[:], in_=primer[:], func=ACT.Silu)
         squares = const.tile([P, V], BF16)
 
         x_codes = keep.tile([P, S_TILES, E_PASSES * P], U32, align_bytes=64)
@@ -72,8 +74,8 @@ def tile_retnet_pc_kernel(tc, x, wg, ret, wo, out):
         weights = {"g": (wg, wg_codes, wg_scales), "o": (wo, wo_codes, wo_scales)}
 
         made = {}
-        taken = {"g": 0, "t": 0, "o": 0}
-        banks = {"g": 4, "t": 2, "o": 2}
+        taken = {"t": 0, "m": 0}
+        banks = {"t": 2, "m": 6}
 
         def load_x(j):
             x_sb = x_in.tile([P, E], BF16)
@@ -206,7 +208,7 @@ def tile_retnet_pc_kernel(tc, x, wg, ret, wo, out):
                 made["rstd", j] = made["roots", b][:, i * HEADS : (i + 1) * HEADS]
 
         def gate_product(j, c):
-            g_bank = g_banks.tile([P, N_TILE], F32)
+            g_bank = m_banks.tile([P, N_TILE], F32, tag="m_bank")
             for g in range(E_PASSES):
                 nc.tensor.matmul_mx(
                     out=g_bank[:],
@@ -218,13 +220,13 @@ def tile_retnet_pc_kernel(tc, x, wg, ret, wo, out):
                     stop=(g == E_PASSES - 1),
                 )
             made["g", j, c] = g_bank
-            taken["g"] += 1
+            taken["m"] += 1
 
         def silu(j, c):
             silu_sb = gate.tile([P, N_TILE], F32)
             nc.scalar.activation(out=silu_sb[:], in_=made["g", j, c][:], func=ACT.Silu)
             made["silu", j, c] = silu_sb
-            taken["g"] -= 1
+            taken["m"] -= 1
 
         def form_h(j, first, last):
             if first == 0:
@@ -287,9 +289,9 @@ def tile_retnet_pc_kernel(tc, x, wg, ret, wo, out):
         def project(j, n, passes):
             codes, scales = made["h_ops", j]
             if passes[0] == 0:
-                o_bank = o_banks.tile([P, N_TILE], F32)
+                o_bank = m_banks.tile([P, N_TILE], F32, tag="m_bank")
                 made["o_bank", j, n] = o_bank
-                taken["o"] += 1
+                taken["m"] += 1
             for c in passes:
                 nc.tensor.matmul_mx(
                     out=made["o_bank", j, n][:],
@@ -309,7 +311,7 @@ def tile_retnet_pc_kernel(tc, x, wg, ret, wo, out):
             nc.sync.dma_start(
                 out=out_rows[j * P : (j + 1) * P, n * N_TILE : (n + 1) * N_TILE], in_=out_sb[:]
             )
-            taken["o"] -= 1
+            taken["m"] -= 1
 
         copies = {"V": nc.vector.tensor_copy, "S": nc.scalar.copy}
 
@@ -324,13 +326,13 @@ def tile_retnet_pc_kernel(tc, x, wg, ret, wo, out):
         def SQ(j, a=0, b=4): return [([("ret", j)], "", sum_squares, (j, 2 * a, 2 * b))]
         def N(b): return ([("sq", j) for j in BATCHES[b]], "", root, (b,))
         def NF(b): return ([("roots", b)], "", finish_root, (b,))
-        def G1(j, c): return ([("xq", j)] + [("wq", "g", c, g) for g in range(E_PASSES)], "g", gate_product, (j, c))
+        def G1(j, c): return ([("xq", j)] + [("wq", "g", c, g) for g in range(E_PASSES)], "m", gate_product, (j, c))
         def SI1(j, c): return ([("g", j, c)], "", silu, (j, c))
         def PR(j, a=0, b=HEADS): return ([("silu", j, c) for c in range(a // 2, b // 2)] + [("rstd", j), ("ret", j)], "", form_h, (j, a, b))
         def HT1(j, b): return ([("h_half", j, b)], "t", turn_h, (j, b))
         def HE1(j, b, e="S"): return ([("h_t", j, b)], "", copy_h, (j, b, copies[e]))
         def HQ(j, halves=(0, 1)): return ([("h_copied", j, b) for b in halves], "", quantise_h, (j, halves))
-        def O1(j, n, passes=(0, 1, 2, 3)): return ([("hq", j, c // 2) for c in passes] + [("wq", "o", n, c) for c in passes], "o" if passes[0] == 0 else "", project, (j, n, passes))
+        def O1(j, n, passes=(0, 1, 2, 3)): return ([("hq", j, c // 2) for c in passes] + [("wq", "o", n, c) for c in passes], "m" if passes[0] == 0 else "", project, (j, n, passes))
         def OE(e, *pairs): return [([("o", j, n)], "", copy_out, (j, n, copies[e])) for j, n in pairs]
         def O(*pairs): return [O1(j, n) for j, n in pairs]
         def W(w, n, cs): return [I(w, n, c) for c in cs] + [Q(w, n, c) for c in cs]
@@ -355,24 +357,24 @@ def tile_retnet_pc_kernel(tc, x, wg, ret, wo, out):
         four = range(4)
         loads = [LW("g", 0, 0), LW("g", 0, 1), LX(0), LX(1), LR(0), LX(2), LX(3), LW("g", 1, 0), LW("g", 1, 1), LR(1), LW("g", 2, 0), LW("g", 2, 1), LX(4), LW("g", 3, 0), LW("g", 3, 1), LX(5), LR(2), LW("o", 0, 0), LW("o", 0, 1), LX(6), LW("o", 0, 2), LW("o", 0, 3), LR(3), LX(7), LW("o", 1, 0), LW("o", 1, 1), LR(4), LR(5), LW("o", 1, 2), LW("o", 1, 3), LR(6), LR(7)]
         vector = W("g", 0, (0, 1)) + [XQ(0), XQ(1), I("g", 1, 0), XQ(2), XQ(3), I("g", 1, 1), Q("g", 1, 0), Q("g", 1, 1)]
-        vector += W("g", 2, (0, 1)) + [N(0)] + W("g", 3, (0, 1))
+        vector += [I("g", 2, 0), N(0), I("g", 2, 1), Q("g", 2, 0), Q("g", 2, 1)] + W("g", 3, (0, 1))
         scalar = [XE(0), XE(1)] + SQ(0, 0, 2) + [XE(2), XE(3)] + SQ(0, 2, 4)
-        scalar += [SI1(j, 0) for j in four] + SQ(1) + [SI1(j, 1) for j in four] + [SI1(j, 2) for j in four] + [XE(4)] + SQ(2, 0, 2) + [SI1(j, 3) for j in four]
+        scalar += SQ(1) + [SI1(j, 0) for j in four] + [SI1(j, 1) for j in four] + [SI1(j, 2) for j in four] + [XE(4)] + SQ(2, 0, 2) + [SI1(j, 3) for j in four]
         tensor = [XT(j) for j in four] + [G1(j, c) for c in (0, 1, 2) for j in four] + [XT(4)] + [G1(j, 3) for j in four] + [XT(5)]
         slots = [
             ([NF(0)] + P2(0) + [XQ(4)], [XE(5)] + SQ(2, 2, 4) + SI(4), G(4)),
-            (P2(1) + [XQ(5)], HE(0), HT(0) + G(5)),
-            (W("o", 0, (0, 1)) + [HQ(0)], HE(1) + SI(5) + [XE(6)], HT(1) + [XT(6)]),
-            (W("o", 0, (2, 3)) + [HQ(1), XQ(6)], SQ(3) + [XE(7)], O((0, 0)) + [XT(7)]),
-            (W("o", 1, (0, 1)) + [XQ(7)], OE("S", (0, 0)) + SI(6) + OE("S", (1, 0)), G(6) + O((1, 0))),
-            ([N(1)] + W("o", 1, (2, 3)), SQ(4) + SQ(5, 0, 2), []),
-            ([NF(1)] + P2(2), SI(7), G(7)),
-            ([PR(3, 0, 4)] + HE(2, "V") + [PR(3, 4, 8)], SQ(5, 2, 4) + OE("S", (0, 1)) + SQ(6), HT(2) + O((0, 1))),
-            ([HQ(2), N(2), NF(2)] + P2(4) + [HE1(3, 0, "V")], SQ(7) + OE("S", (1, 1)) + [HE1(3, 1)], O((1, 1)) + HT(3) + O((2, 0))),
-            ([N(3), HQ(3)] + P2(5), OE("S", (2, 0)) + HE(4) + OE("S", (2, 1)), HT(4) + O((2, 1), (3, 0))),
-            ([HQ(4), NF(3)] + P2(6), OE("S", (3, 0)) + HE(5) + OE("S", (3, 1)), O((3, 1)) + HT(5) + O((4, 0))),
-            ([HQ(5)] + P2(7), OE("S", (4, 0), (4, 1)) + HE(6), O((4, 1)) + HT(6) + O((5, 0))),
-            ([HQ(6)] + OE("V", (5, 1)), OE("S", (5, 0)) + HE(7), HT(7) + O((5, 1))),
+            (P2(1) + [XQ(5)], HE(0) + SQ(3, 0, 2), HT(0)),
+            (W("o", 0, (0, 1)) + [HQ(0)], HE(1) + SQ(3, 2, 4) + [XE(6)], HT(1) + [XT(6)] + G(5)),
+            (W("o", 0, (2, 3)) + [HQ(1), XQ(6)], SQ(4) + [XE(7)], [XT(7)] + O((0, 0))),
+            ([I("o", 1, 0), N(1), I("o", 1, 1), Q("o", 1, 0), Q("o", 1, 1), XQ(7)], SI(5) + OE("S", (0, 0)), O((1, 0))),
+            (W("o", 1, (2, 3)), SI(6) + OE("S", (1, 0)) + SQ(5, 0, 2), G(6)),
+            ([NF(1)] + P2(2), SQ(5, 2, 4) + SQ(6, 0, 2), O((0, 1), (1, 1))),
+            ([PR(3, 0, 4)] + HE(2, "V") + [PR(3, 4, 8)], SQ(6, 2, 4) + SQ(7), HT(2)),
+            ([HQ(2), N(2), PR(4, 0, 4), PR(4, 4, 8)], HE(3) + OE("S", (0, 1)) + SI(7), HT(3) + G(7) + O((2, 0), (2, 1))),
+            ([HQ(3), NF(2), PR(5, 0, 4), PR(5, 4, 8)], OE("S", (1, 1)) + HE(4) + OE("S", (2, 0), (2, 1)), HT(4) + O((3, 0))),
+            ([PR(6, 0, 4), HQ(4), PR(6, 4, 8)], HE(5) + OE("S", (3, 0), (3, 1)), HT(5) + O((3, 1), (4, 0))),
+            ([HQ(5), PR(7, 0, 4), PR(7, 4, 6), HQ(6), PR(7, 6, 8)], HE(6) + OE("S", (4, 0), (4, 1)), HT(6) + O((4, 1), (5, 0))),
+            (OE("V", (5, 1)), HE(7) + OE("S", (5, 0)), [HT1(7, 0)] + O((5, 1)) + [HT1(7, 1)]),
             ([HQ(7, (0,)), HQ(7, (1,))] + OE("V", (6, 1)), OE("S", (6, 0)), O((6, 0), (6, 1)) + [O1(7, 0, (0, 1)), O1(7, 0, (2, 3)), O1(7, 1, (0, 1)), O1(7, 1, (2, 3))]),
             (OE("V", (7, 1)), OE("S", (7, 0)), []),
         ]

@@ -370,9 +370,9 @@ def tile_retnet_pc_kernel(tc, x, wg, ret, wo, out):
             (W("o", 1, (2, 3)), SI(6) + OE("S", (1, 0)) + SQ(5, 0, 2), G(6)),
             ([NF(1)] + P2(2), SQ(5, 2, 4) + SQ(6, 0, 2), O((0, 1), (1, 1))),
             ([PR(3, 0, 4)] + HE(2, "V") + [PR(3, 4, 8)], SQ(6, 2, 4) + SQ(7), HT(2)),
-            ([HQ(2), N(2), PR(4, 0, 4), PR(4, 4, 8)], HE(3) + OE("S", (0, 1)) + SI(7), HT(3) + G(7) + O((2, 0), (2, 1))),
-            ([HQ(3), NF(2), PR(5, 0, 4), PR(5, 4, 8)], OE("S", (1, 1)) + HE(4) + OE("S", (2, 0), (2, 1)), HT(4) + O((3, 0))),
-            ([PR(6, 0, 4), HQ(4), PR(6, 4, 8)], HE(5) + OE("S", (3, 0), (3, 1)), HT(5) + O((3, 1), (4, 0))),
+            ([HQ(2), N(2), PR(4, 0, 4), PR(4, 4, 8)], HE(3) + OE("S", (0, 1)) + SI(7), HT(3) + G(7) + O((2, 0))),
+            ([HQ(3), NF(2), PR(5, 0, 4), PR(5, 4, 8)], OE("S", (1, 1)) + HE(4) + OE("S", (2, 0), (2, 1)), HT(4) + O((2, 1), (3, 0))),
+            ([HQ(4), PR(6, 0, 4), PR(6, 4, 8)], HE(5) + OE("S", (3, 0), (3, 1)), HT(5) + O((3, 1), (4, 0))),
             ([HQ(5), PR(7, 0, 4), PR(7, 4, 6), HQ(6), PR(7, 6, 8)], HE(6) + OE("S", (4, 0), (4, 1)), HT(6) + O((4, 1), (5, 0))),
             (OE("V", (5, 1)), HE(7) + OE("S", (5, 0)), [HT1(7, 0)] + O((5, 1)) + [HT1(7, 1)]),
             ([HQ(7, (0,)), HQ(7, (1,))] + OE("V", (6, 1)), OE("S", (6, 0)), O((6, 0), (6, 1)) + [O1(7, 0, (0, 1)), O1(7, 0, (2, 3)), O1(7, 1, (0, 1)), O1(7, 1, (2, 3))]),

@@ -248,9 +248,14 @@ def tile_retnet_pc_kernel(tc, x, wg, ret, wo, out):
             if last - first == HEADS:
                 made["h_half", j, 0] = True
 
-        def turn_h(j, b):
+        def turn_h(j, b, warm):
             h_words = made["h", j][:].bitcast(F32)
             h_t = t_banks.tile([P, N_TILE], F32, tag="t_bank")
+            for i in range(warm):
+                nc.tensor.matmul(
+                    out=h_t[:], lhsT=made["ret", j][:, :P], rhs=made["ret", j][:, :N_TILE],
+                    start=True, stop=True,
+                )
             for a in range(4):
                 w0 = (4 * b + a) * P
                 nc.tensor.transpose(h_t[:, a * P : (a + 1) * P], h_words[:, w0 : w0 + P], ident[:])
@@ -329,7 +334,7 @@ def tile_retnet_pc_kernel(tc, x, wg, ret, wo, out):
         def G1(j, c): return ([("xq", j)] + [("wq", "g", c, g) for g in range(E_PASSES)], "m", gate_product, (j, c))
         def SI1(j, c): return ([("g", j, c)], "", silu, (j, c))
         def PR(j, a=0, b=HEADS): return ([("silu", j, c) for c in range(a // 2, b // 2)] + [("rstd", j), ("ret", j)], "", form_h, (j, a, b))
-        def HT1(j, b): return ([("h_half", j, b)], "t", turn_h, (j, b))
+        def HT1(j, b, warm=0): return ([("h_half", j, b)], "t", turn_h, (j, b, warm))
         def HE1(j, b, e="S"): return ([("h_t", j, b)], "", copy_h, (j, b, copies[e]))
         def HQ(j, halves=(0, 1)): return ([("h_copied", j, b) for b in halves], "", quantise_h, (j, halves))
         def O1(j, n, passes=(0, 1, 2, 3)): return ([("hq", j, c // 2) for c in passes] + [("wq", "o", n, c) for c in passes], "m" if passes[0] == 0 else "", project, (j, n, passes))
@@ -369,11 +374,11 @@ def tile_retnet_pc_kernel(tc, x, wg, ret, wo, out):
             ([I("o", 1, 0), N(1), I("o", 1, 1), Q("o", 1, 0), Q("o", 1, 1), XQ(7)], SI(5) + OE("S", (0, 0)), O((1, 0))),
             (W("o", 1, (2, 3)), SI(6) + OE("S", (1, 0)) + SQ(5, 0, 2), G(6)),
             ([NF(1)] + P2(2), SQ(5, 2, 4) + SQ(6, 0, 2), O((0, 1), (1, 1))),
-            ([PR(3, 0, 4)] + HE(2, "V") + [PR(3, 4, 8)], SQ(6, 2, 4) + SQ(7), HT(2)),
-            ([HQ(2), N(2), PR(4, 0, 4), PR(4, 4, 8)], HE(3) + OE("S", (0, 1)) + SI(7), HT(3) + G(7) + O((2, 0))),
-            ([HQ(3), NF(2), PR(5, 0, 4), PR(5, 4, 8)], OE("S", (1, 1)) + HE(4) + OE("S", (2, 0), (2, 1)), HT(4) + O((2, 1), (3, 0))),
-            ([HQ(4), PR(6, 0, 4), PR(6, 4, 8)], HE(5) + OE("S", (3, 0), (3, 1)), HT(5) + O((3, 1), (4, 0))),
-            ([HQ(5), PR(7, 0, 4), PR(7, 4, 6), HQ(6), PR(7, 6, 8)], HE(6) + OE("S", (4, 0), (4, 1)), HT(6) + O((4, 1), (5, 0))),
+            ([PR(3, 0, 4)] + HE(2, "V") + [PR(3, 4, 8)], SQ(6, 2, 4) + SQ(7), [HT1(2, 0), G1(7, 0), G1(7, 1), HT1(2, 1), G1(7, 2), G1(7, 3)]),
+            ([HQ(2), N(2), PR(4, 0, 4), PR(4, 4, 8)], [HE1(3, 0)] + OE("S", (0, 1)) + [HE1(3, 1)] + OE("S", (1, 1)) + SI(7)[:2], [HT1(3, 0, 3), HT1(3, 1, 3)] + O((2, 0), (2, 1))),
+            ([HQ(3), NF(2), PR(5, 0, 4), PR(5, 4, 8)], HE(4) + SI(7)[2:] + OE("S", (2, 0), (2, 1)), HT(4) + O((3, 0))),
+            ([HQ(4), PR(6, 0, 4), PR(6, 4, 6), HQ(5), PR(6, 6, 8)], HE(5) + OE("S", (3, 0), (3, 1)), O((3, 1)) + HT(5) + O((4, 0))),
+            ([PR(7, 0, 4), PR(7, 4, 6), HQ(6), PR(7, 6, 8)], HE(6) + OE("S", (4, 0), (4, 1)), O((4, 1)) + HT(6) + O((5, 0))),
             (OE("V", (5, 1)), HE(7) + OE("S", (5, 0)), [HT1(7, 0)] + O((5, 1)) + [HT1(7, 1)]),
             ([HQ(7, (0,)), HQ(7, (1,))] + OE("V", (6, 1)), OE("S", (6, 0)), O((6, 0), (6, 1)) + [O1(7, 0, (0, 1)), O1(7, 0, (2, 3)), O1(7, 1, (0, 1)), O1(7, 1, (2, 3))]),
             (OE("V", (7, 1)), OE("S", (7, 0)), []),

import concourse.mybir as mybir
from concourse.masks import make_identity

F32 = mybir.dt.float32
BF16 = mybir.dt.bfloat16
U32 = mybir.dt.uint32
U8 = mybir.dt.uint8
I32 = mybir.dt.int32
FP8X4 = mybir.dt.float8_e4m3fn_x4
ACT = mybir.ActivationFunctionType
ALU = mybir.AluOpType

P = 128
S, E, V = 1024, 1024, 2048
HEADS, HEAD_DIM = 8, 256
EPS = 1e-5
PACK = 4
K_PASS = P * PACK
N_TILE = 512
S_TILES = S // P
E_PASSES = E // K_PASS
V_PASSES = V // K_PASS
V_CHUNKS = V // N_TILE
E_CHUNKS = E // N_TILE
HEADS_PER_CHUNK = N_TILE // HEAD_DIM
BATCHES = ((0, 1), (2, 3, 4), (5, 6, 7))
RSQRT_GUESS = 0x5F3759DF - (1 << 22)
FLOPS = 2 * S * E * V + 2 * S * V * E


def regroup(copy, grouped, planes):
    copy(
        out=grouped.rearrange("p (c i t) -> p c t i", i=4, t=PACK),
        in_=planes.rearrange("p t (c i) -> p c t i", i=4),
    )


def tile_retnet_pc_kernel(tc, x, wg, ret, wo, out):
    nc = tc.nc
    x_rows = x.flatten_outer_dims()
    ret_rows = ret.rearrange("b s h d -> (b s) (h d)")
    out_rows = out.flatten_outer_dims()

    with (
        tc.tile_pool(name="const", bufs=1) as const,
        tc.tile_pool(name="x_in", bufs=6) as x_in,
        tc.tile_pool(name="ret_in", bufs=S_TILES) as ret_in,
        tc.tile_pool(name="w_in", bufs=8) as w_in,
        tc.tile_pool(name="keep", bufs=1) as keep,
        tc.tile_pool(name="group", bufs=3) as group,
        tc.tile_pool(name="gate", bufs=24) as gate,
        tc.tile_pool(name="stats", bufs=2) as stats,
        tc.tile_pool(name="x_pairs", bufs=3) as x_pairs,
        tc.tile_pool(name="h_pairs", bufs=2) as h_pairs,
        tc.tile_pool(name="work", bufs=2) as work,
        tc.tile_pool(name="h_ops", bufs=6) as h_ops,
        tc.tile_pool(name="store", bufs=5) as store,
        tc.psum_pool(name="t_banks", bufs=2) as t_banks,
        tc.psum_pool(name="m_banks", bufs=6) as m_banks,
    ):
        ident = const.tile([P, P], F32)
        make_identity(nc, ident[:])
        primer = const.tile([P, 1], F32)
        nc.vector.memset(primer[:], 0.0)
        nc.scalar.activation(out=primer[:], in_=primer[:], func=ACT.Silu)
        squares = const.tile([P, V], BF16)

        x_codes = keep.tile([P, S_TILES, E_PASSES * P], U32, align_bytes=64)
        x_scales = keep.tile([P, S_TILES, E_PASSES * P], U8, align_bytes=64)
        wg_codes = keep.tile([P, E_PASSES, V], U32, align_bytes=64)
        wg_scales = keep.tile([P, E_PASSES, V], U8, align_bytes=64)
        wo_codes = keep.tile([P, V_PASSES, E], U32, align_bytes=64)
        wo_scales = keep.tile([P, V_PASSES, E], U8, align_bytes=64)
        weights = {"g": (wg, wg_codes, wg_scales), "o": (wo, wo_codes, wo_scales)}

        made = {}
        taken = {"t": 0, "m": 0}
        banks = {"t": 2, "m": 6}

        def load_x(j):
            x_sb = x_in.tile([P, E], BF16)
            nc.sync.dma_start(out=x_sb[:], in_=x_rows[j * P : (j + 1) * P, :])
            made["x", j] = x_sb

        def load_ret(j):
            ret_sb = ret_in.tile([P, V], BF16)
            nc.sync.dma_start(out=ret_sb[:], in_=ret_rows[j * P : (j + 1) * P, :])
            made["ret", j] = ret_sb

        def load_w(w, n, c):
            w_raw = w_in.tile([P, PACK * N_TILE], BF16)
            planes = w_raw[:].rearrange("p (u e v) -> p u e v", u=2, e=2)
            rows = weights[w][0][c * K_PASS : (c + 1) * K_PASS, n * N_TILE : (n + 1) * N_TILE]
            rows = rows.rearrange("(u q e) v -> u q e v", u=2, e=2)
            for u in range(2):
                nc.sync.dma_start(out=planes[:, u, :, :], in_=rows[u])
            made["raw", w, n, c] = w_raw

        def turn_x(j):
            x_words = made["x", j][:].bitcast(F32)
            x_t = t_banks.tile([P, N_TILE], F32, tag="t_bank")
            for a in range(2 * E_PASSES):
                nc.tensor.transpose(
                    x_t[:, a * P : (a + 1) * P], x_words[:, a * P : (a + 1) * P], ident[:]
                )
            made["x_t", j] = x_t
            taken["t"] += 1

        def copy_x(j, copy):
            x_grouped = x_pairs.tile([P, E], BF16, align_bytes=64)
            copy(
                out=x_grouped[:].bitcast(F32).rearrange("p (g s u) -> p g s u", g=E_PASSES, u=2),
                in_=made["x_t", j][:].rearrange("p (g u s) -> p g s u", g=E_PASSES, u=2),
            )
            made["x_grouped", j] = x_grouped
            taken["t"] -= 1

        def quantise_x(j):
            nc.vector.quantize_mx(
                out=x_codes[:, j, :].bitcast(FP8X4), scales=x_scales[:, j, :],
                in_=made["x_grouped", j][:],
            )
            made["xq", j] = True
            next_small(1)

        def group_w(w, n, c):
            grouped = group.tile([P, PACK * N_TILE], BF16, align_bytes=64)
            planes = made["raw", w, n, c][:].rearrange("p (t v) -> p t v", t=PACK)
            regroup(nc.vector.tensor_copy, grouped[:], planes)
            made["grouped", w, n, c] = grouped
            next_small(1)

        def quantise_w(w, n, c):
            cols = slice(n * N_TILE, (n + 1) * N_TILE)
            nc.vector.quantize_mx(
                out=weights[w][1][:, c, cols].bitcast(FP8X4),
                scales=weights[w][2][:, c, cols],
                in_=made["grouped", w, n, c][:],
            )
            made["wq", w, n, c] = True
            next_small(1)

        def sum_squares(j, first, last):
            if ("sumsq", j) not in made:
                b = [j in batch for batch in BATCHES].index(True)
                sumsq = stats.tile([P, len(BATCHES[b]) * HEADS], F32)
                made["sumsq_all", b] = sumsq
                for i, tile in enumerate(BATCHES[b]):
                    made["sumsq", tile] = sumsq[:, i * HEADS : (i + 1) * HEADS]
            for h in range(first, last):
                cols = slice(h * HEAD_DIM, (h + 1) * HEAD_DIM)
                nc.scalar.activation(
                    out=squares[:, cols],
                    in_=made["ret", j][:, cols],
                    func=ACT.Square,
                    accum_out=made["sumsq", j][:, h : h + 1],
                )
            if last == HEADS:
                made["sq", j] = True

        def root(b):
            width = len(BATCHES[b]) * HEADS
            half = stats.tile([P, width], F32)
            rstd = stats.tile([P, width], I32)
            square = stats.tile([P, width], F32)
            rest = stats.tile([P, width], F32)
            y = rstd[:].bitcast(F32)

            def first():
                nc.vector.tensor_scalar(
                    out=half[:], in0=made["sumsq_all", b][:], scalar1=0.5 / HEAD_DIM,
                    scalar2=0.5 * EPS, op0=ALU.mult, op1=ALU.add,
                )

            def guess():
                nc.vector.tensor_scalar(
                    out=rstd[:], in0=half[:].bitcast(I32), scalar1=-0.5, scalar2=float(RSQRT_GUESS),
                    op0=ALU.mult, op1=ALU.add,
                )

            def multiply():
                nc.vector.tensor_tensor(out=square[:], in0=y, in1=y, op=ALU.mult)

            def negate():
                nc.vector.scalar_tensor_tensor(
                    out=rest[:], in0=square[:], scalar=-1.0, in1=half[:],
                    op0=ALU.mult, op1=ALU.mult,
                )

            def improve():
                nc.vector.scalar_tensor_tensor(
                    out=y, in0=rest[:], scalar=1.5, in1=y, op0=ALU.add, op1=ALU.mult
                )

            small.extend([first, guess] + 3 * [multiply, negate, improve])
            made["roots", b] = y

        small = []

        def next_small(count):
            for i in range(count):
                if small:
                    small.pop(0)()

        def finish_root(b):
            next_small(len(small))
            for i, j in enumerate(BATCHES[b]):
                made["rstd", j] = made["roots", b][:, i * HEADS : (i + 1) * HEADS]

        def gate_product(j, c):
            g_bank = m_banks.tile([P, N_TILE], F32, tag="m_bank")
            for g in range(E_PASSES):
                nc.tensor.matmul_mx(
                    out=g_bank[:],
                    lhsT=x_codes[:, j, g * P : (g + 1) * P].bitcast(FP8X4),
                    lhsT_scale=x_scales[:, j, g * P : (g + 1) * P],
                    rhs=wg_codes[:, g, c * N_TILE : (c + 1) * N_TILE].bitcast(FP8X4),
                    rhs_scale=wg_scales[:, g, c * N_TILE : (c + 1) * N_TILE],
                    start=(g == 0),
                    stop=(g == E_PASSES - 1),
                )
            made["g", j, c] = g_bank
            taken["m"] += 1

        def silu(j, c):
            silu_sb = gate.tile([P, N_TILE], F32)
            nc.scalar.activation(out=silu_sb[:], in_=made["g", j, c][:], func=ACT.Silu)
            made["silu", j, c] = silu_sb
            taken["m"] -= 1

        def form_h(j, first, last):
            if first == 0:
                h_sb = work.tile([P, V], BF16)
                made["h", j] = h_sb
            for h in range(first, last):
                cols = slice(h * HEAD_DIM, (h + 1) * HEAD_DIM)
                part = slice((h % HEADS_PER_CHUNK) * HEAD_DIM, (h % HEADS_PER_CHUNK + 1) * HEAD_DIM)
                nc.vector.scalar_tensor_tensor(
                    out=made["h", j][:, cols],
                    in0=made["silu", j, h // HEADS_PER_CHUNK][:, part],
                    scalar=made["rstd", j][:, h : h + 1],
                    in1=made["ret", j][:, cols],
                    op0=ALU.mult,
                    op1=ALU.mult,
                )
                next_small(1)
            made["h_half", j, last // 4 - 1] = True
            if last - first == HEADS:
                made["h_half", j, 0] = True

        def turn_h(j, b, warm):
            h_words = made["h", j][:].bitcast(F32)
            h_t = t_banks.tile([P, N_TILE], F32, tag="t_bank")
            for i in range(warm):
                nc.tensor.matmul(
                    out=h_t[:], lhsT=made["ret", j][:, :P], rhs=made["ret", j][:, :N_TILE],
                    start=True, stop=True,
                )
            for a in range(4):
                w0 = (4 * b + a) * P
                nc.tensor.transpose(h_t[:, a * P : (a + 1) * P], h_words[:, w0 : w0 + P], ident[:])
            made["h_t", j, b] = h_t
            taken["t"] += 1

        def copy_h(j, b, copy):
            if ("h_grouped", j) not in made:
                h_grouped = h_pairs.tile([P, V], BF16, align_bytes=64)
                made["h_grouped", j] = h_grouped
            copy(
                out=made["h_grouped", j][:].bitcast(F32)[:, b * N_TILE : (b + 1) * N_TILE].rearrange(
                    "p (c s u) -> p c s u", c=2, u=2
                ),
                in_=made["h_t", j, b][:].rearrange("p (c u s) -> p c s u", c=2, u=2),
            )
            made["h_copied", j, b] = True
            taken["t"] -= 1

        def quantise_h(j, halves):
            if 0 in halves:
                h_codes = h_ops.tile([P, V_PASSES * P], U32, align_bytes=64)
                h_scales = h_ops.tile([P, V_PASSES * P], U8, align_bytes=64)
                made["h_ops", j] = (h_codes, h_scales)
            codes, scales = made["h_ops", j]
            words = slice(halves[0] * 2 * P, (halves[-1] + 1) * 2 * P)
            values = slice(halves[0] * V // 2, (halves[-1] + 1) * V // 2)
            nc.vector.quantize_mx(
                out=codes[:, words].bitcast(FP8X4), scales=scales[:, words],
                in_=made["h_grouped", j][:, values],
            )
            for b in halves:
                made["hq", j, b] = True
            next_small(1)

        def project(j, n, passes):
            codes, scales = made["h_ops", j]
            if passes[0] == 0:
                o_bank = m_banks.tile([P, N_TILE], F32, tag="m_bank")
                made["o_bank", j, n] = o_bank
                taken["m"] += 1
            for c in passes:
                nc.tensor.matmul_mx(
                    out=made["o_bank", j, n][:],
                    lhsT=codes[:, c * P : (c + 1) * P].bitcast(FP8X4),
                    lhsT_scale=scales[:, c * P : (c + 1) * P],
                    rhs=wo_codes[:, c, n * N_TILE : (n + 1) * N_TILE].bitcast(FP8X4),
                    rhs_scale=wo_scales[:, c, n * N_TILE : (n + 1) * N_TILE],
                    start=(c == 0),
                    stop=(c == V_PASSES - 1),
                )
            if passes[-1] == V_PASSES - 1:
                made["o", j, n] = True

        def copy_out(j, n, copy):
            out_sb = store.tile([P, N_TILE], F32)
            copy(out=out_sb[:], in_=made["o_bank", j, n][:])
            nc.sync.dma_start(
                out=out_rows[j * P : (j + 1) * P, n * N_TILE : (n + 1) * N_TILE], in_=out_sb[:]
            )
            taken["m"] -= 1

        copies = {"V": nc.vector.tensor_copy, "S": nc.scalar.copy}

        def LX(j): return ([], "", load_x, (j,))
        def LR(j): return ([], "", load_ret, (j,))
        def LW(w, n, c): return ([], "", load_w, (w, n, c))
        def XT(j): return ([("x", j)], "t", turn_x, (j,))
        def XE(j, e="S"): return ([("x_t", j)], "", copy_x, (j, copies[e]))
        def XQ(j): return ([("x_grouped", j)], "", quantise_x, (j,))
        def I(w, n, c): return ([("raw", w, n, c)], "", group_w, (w, n, c))
        def Q(w, n, c): return ([("grouped", w, n, c)], "", quantise_w, (w, n, c))
        def SQ(j, a=0, b=4): return [([("ret", j)], "", sum_squares, (j, 2 * a, 2 * b))]
        def N(b): return ([("sq", j) for j in BATCHES[b]], "", root, (b,))
        def NF(b): return ([("roots", b)], "", finish_root, (b,))
        def G1(j, c): return ([("xq", j)] + [("wq", "g", c, g) for g in range(E_PASSES)], "m", gate_product, (j, c))
        def SI1(j, c): return ([("g", j, c)], "", silu, (j, c))
        def PR(j, a=0, b=HEADS): return ([("silu", j, c) for c in range(a // 2, b // 2)] + [("rstd", j), ("ret", j)], "", form_h, (j, a, b))
        def HT1(j, b, warm=0): return ([("h_half", j, b)], "t", turn_h, (j, b, warm))
        def HE1(j, b, e="S"): return ([("h_t", j, b)], "", copy_h, (j, b, copies[e]))
        def HQ(j, halves=(0, 1)): return ([("h_copied", j, b) for b in halves], "", quantise_h, (j, halves))
        def O1(j, n, passes=(0, 1, 2, 3)): return ([("hq", j, c // 2) for c in passes] + [("wq", "o", n, c) for c in passes], "m" if passes[0] == 0 else "", project, (j, n, passes))
        def OE(e, *pairs): return [([("o", j, n)], "", copy_out, (j, n, copies[e])) for j, n in pairs]
        def O(*pairs): return [O1(j, n) for j, n in pairs]
        def W(w, n, cs): return [I(w, n, c) for c in cs] + [Q(w, n, c) for c in cs]
        def SI(j): return [SI1(j, c) for c in four]
        def G(j): return [G1(j, c) for c in four]
        def HE(j, e="S"): return [HE1(j, 0, e), HE1(j, 1, e)]
        def HT(j): return [HT1(j, 0), HT1(j, 1)]
        def P2(j): return [PR(j, 0, 4), PR(j, 4, 8)]

        def issue(programs):
            while any(programs):
                moved = False
                for program in programs:
                    if program:
                        names, bank, step, arguments = program[0]
                        if all([name in made for name in names]) and (not bank or taken[bank] < banks[bank]):
                            step(*arguments)
                            program.pop(0)
                            moved = True
                assert moved

        four = range(4)
        loads = [LW("g", 0, 0), LW("g", 0, 1), LX(0), LX(1), LR(0), LX(2), LX(3), LW("g", 1, 0), LW("g", 1, 1), LR(1), LW("g", 2, 0), LW("g", 2, 1), LX(4), LW("g", 3, 0), LW("g", 3, 1), LX(5), LR(2), LW("o", 0, 0), LW("o", 0, 1), LX(6), LW("o", 0, 2), LW("o", 0, 3), LR(3), LX(7), LW("o", 1, 0), LW("o", 1, 1), LR(4), LR(5), LW("o", 1, 2), LW("o", 1, 3), LR(6), LR(7)]
        vector = W("g", 0, (0, 1)) + [XQ(0), XQ(1), I("g", 1, 0), XQ(2), XQ(3), I("g", 1, 1), Q("g", 1, 0), Q("g", 1, 1)]
        vector += [I("g", 2, 0), N(0), I("g", 2, 1), Q("g", 2, 0), Q("g", 2, 1)] + W("g", 3, (0, 1))
        scalar = [XE(0), XE(1)] + SQ(0, 0, 2) + [XE(2), XE(3)] + SQ(0, 2, 4)
        scalar += SQ(1) + [SI1(j, 0) for j in four] + [SI1(j, 1) for j in four] + [SI1(j, 2) for j in four] + [XE(4)] + SQ(2, 0, 2) + [SI1(j, 3) for j in four]
        tensor = [XT(j) for j in four] + [G1(j, c) for c in (0, 1, 2) for j in four] + [XT(4)] + [G1(j, 3) for j in four] + [XT(5)]
        slots = [
            ([NF(0)] + P2(0) + [XQ(4)], [XE(5)] + SQ(2, 2, 4) + SI(4), G(4)),
            (P2(1) + [XQ(5)], HE(0) + SQ(3, 0, 2), HT(0)),
            (W("o", 0, (0, 1)) + [HQ(0)], HE(1) + SQ(3, 2, 4) + [XE(6)], HT(1) + [XT(6)] + G(5)),
            (W("o", 0, (2, 3)) + [HQ(1), XQ(6)], SQ(4) + [XE(7)], [XT(7)] + O((0, 0))),
            ([I("o", 1, 0), N(1), I("o", 1, 1), Q("o", 1, 0), Q("o", 1, 1), XQ(7)], SI(5) + OE("S", (0, 0)), O((1, 0))),
            (W("o", 1, (2, 3)), SI(6) + OE("S", (1, 0)) + SQ(5, 0, 2), G(6)),
            ([NF(1)] + P2(2), SQ(5, 2, 4) + SQ(6, 0, 2), O((0, 1), (1, 1))),
            ([PR(3, 0, 4)] + HE(2, "V") + [PR(3, 4, 8)], SQ(6, 2, 4) + SQ(7), [HT1(2, 0), G1(7, 0), G1(7, 1), HT1(2, 1), G1(7, 2), G1(7, 3)]),
            ([HQ(2), N(2), PR(4, 0, 4), PR(4, 4, 8)], [HE1(3, 0)] + OE("S", (0, 1)) + [HE1(3, 1)] + OE("S", (1, 1)) + SI(7)[:2], [HT1(3, 0, 3), HT1(3, 1, 3)] + O((2, 0), (2, 1))),
            ([HQ(3), NF(2), PR(5, 0, 4), PR(5, 4, 8)], HE(4) + SI(7)[2:] + OE("S", (2, 0), (2, 1)), HT(4) + O((3, 0))),
            ([HQ(4), PR(6, 0, 4), PR(6, 4, 6), HQ(5), PR(6, 6, 8)], HE(5) + OE("S", (3, 0), (3, 1)), O((3, 1)) + HT(5) + O((4, 0))),
            ([PR(7, 0, 4), PR(7, 4, 6), HQ(6), PR(7, 6, 8)], HE(6) + OE("S", (4, 0), (4, 1)), O((4, 1)) + HT(6) + O((5, 0))),
            (OE("V", (5, 1)), HE(7) + OE("S", (5, 0)), [HT1(7, 0)] + O((5, 1)) + [HT1(7, 1)]),
            ([HQ(7, (0,)), HQ(7, (1,))] + OE("V", (6, 1)), OE("S", (6, 0)), O((6, 0), (6, 1)) + [O1(7, 0, (0, 1)), O1(7, 0, (2, 3)), O1(7, 1, (0, 1)), O1(7, 1, (2, 3))]),
            (OE("V", (7, 1)), OE("S", (7, 0)), []),
        ]
        for v, s, p in slots:
            vector += v
            scalar += s
            tensor += p
        with tc.manual_schedule():
            issue([loads, vector, tensor, scalar])
